import numpy as np
import ml_dtypes


def mxq(x, axis, fmt="e4m3"):
    dtype, down = {"e4m3": (ml_dtypes.float8_e4m3fn, 7), "e5m2": (ml_dtypes.float8_e5m2, 14)}[fmt]
    v = np.moveaxis(np.asarray(x, np.float32).astype(ml_dtypes.bfloat16).astype(np.float64), axis, -1)
    blocks = v.reshape(v.shape[:-1] + (-1, 32))
    amax = np.abs(blocks).max(-1, keepdims=True)
    byte = np.maximum(np.where(amax > 0, np.frexp(amax)[1] - 1 + 127, 0) - down, 1)
    scale = np.exp2(byte - 127.0)
    codes = (blocks / scale).astype(np.float32).astype(dtype).astype(np.float64)
    return np.moveaxis((codes * scale).reshape(v.shape), -1, axis)


WIDE = False


def mx_kscale(k):
    if not WIDE:
        return np.ones(k)
    levels = np.array([10, -10, 5, -5, 0])
    a = np.random.permutation(np.resize(levels, k // 512 * 4)).reshape(k // 512, 4)
    idx = np.arange(k)
    return np.exp2(a[idx // 512, idx % 128 // 32])


BF16 = ml_dtypes.bfloat16


def bf(x):
    return np.asarray(x, np.float32).astype(BF16)


def f64(x):
    return np.asarray(x).astype(np.float64)


E2M1 = np.array([0.0, 0.5, 1.0, 1.5, 2.0, 3.0, 4.0, 6.0, -0.0, -0.5, -1.0, -1.5, -2.0, -3.0, -4.0, -6.0])


def pack_weight(w, fmt):
    k, n = w.shape
    w = f64(bf(w)).reshape(k // 32, 32, n)
    amax = np.abs(w).max(1)
    if fmt == "e4m3":
        byte = np.frexp(amax)[1] - 1 + 127 - 7
    else:
        mant, ex = np.frexp(amax / 6.0)
        byte = np.where(mant > 0.5, ex, ex - 1) + 127
    byte = np.clip(np.where(amax > 0, byte, 1), 1, 254)
    scaled = (w * np.exp2(127.0 - byte)[:, None, :]).reshape(k, n).astype(np.float32)
    by_word = np.ascontiguousarray(scaled.reshape(k // 512, 128, 4, n).transpose(0, 1, 3, 2))
    if fmt == "e4m3":
        words = by_word.astype(ml_dtypes.float8_e4m3fn).view(np.uint8)
    else:
        c = by_word.astype(ml_dtypes.float4_e2m1fn).view(np.uint8) & 0xF
        words = c[..., 0::2] | (c[..., 1::2] << 4)
    return np.ascontiguousarray(words), np.ascontiguousarray(byte.astype(np.uint8).reshape(k // 512, 16, n))


def unpack_weight(words, scales, fmt):
    g, p, n, _ = words.shape
    if fmt == "e4m3":
        vals = np.ascontiguousarray(words).view(ml_dtypes.float8_e4m3fn).astype(np.float64)
    else:
        nib = np.empty((g, p, n, 4), np.uint8)
        nib[..., 0::2] = words & 0xF
        nib[..., 1::2] = words >> 4
        vals = E2M1[nib]
    vals = vals * np.repeat(np.exp2(scales.astype(np.float64) - 127.0), 8, axis=1)[..., None]
    return vals.transpose(0, 1, 3, 2).reshape(g * 512, n)


B, L, C, H, W, HID = 2, 2, 512, 16, 16, 4096
BLK = 32
FMT = "e4m3"


def silu(v):
    return v / (1.0 + np.exp(-v))


def _dwt(x):
    x1 = x[:, :, 0::2, 0::2] * 0.5
    x2 = x[:, :, 1::2, 0::2] * 0.5
    x3 = x[:, :, 0::2, 1::2] * 0.5
    x4 = x[:, :, 1::2, 1::2] * 0.5
    return np.concatenate([x1 + x2 + x3 + x4,
                           -x1 - x2 + x3 + x4,
                           -x1 + x2 - x3 + x4,
                           x1 - x2 - x3 + x4], axis=1)


def _idwt(y):
    n, c4, hh, wh = y.shape
    co = c4 // 4
    y1 = y[:, 0 * co:1 * co] * 0.5
    y2 = y[:, 1 * co:2 * co] * 0.5
    y3 = y[:, 2 * co:3 * co] * 0.5
    y4 = y[:, 3 * co:4 * co] * 0.5
    a = y1 - y2 - y3 + y4
    b = y1 - y2 + y3 - y4
    c = y1 + y2 - y3 - y4
    d = y1 + y2 + y3 + y4
    r0 = np.stack([a, c], axis=-1).reshape(n, co, hh, 2 * wh)
    r1 = np.stack([b, d], axis=-1).reshape(n, co, hh, 2 * wh)
    return np.stack([r0, r1], axis=-2).reshape(n, co, 2 * hh, 2 * wh)


def setup_inputs():
    f = np.sort(mx_kscale(4 * C)[::BLK])
    s = np.repeat(f[np.round(np.linspace(0, f.size - 1, C // BLK)).astype(int)], BLK)
    s4 = np.tile(s, 4)
    x = bf(np.random.standard_normal((B, L, C, H, W)) * s[:, None, None])
    conv_w = np.random.standard_normal((HID, 4 * C)) / np.sqrt(4 * C) / s4[None, :]
    conv_w_words, conv_w_scales = pack_weight(np.ascontiguousarray(conv_w.T), FMT)
    conv_b = bf(np.random.standard_normal(HID) * 0.3)
    conv_out_w = np.random.standard_normal((4 * C, HID)) * 1.5 / np.sqrt(HID)
    conv_out_w_words, conv_out_w_scales = pack_weight(np.ascontiguousarray(conv_out_w.T), FMT)
    conv_out_b = bf(np.random.standard_normal(4 * C) * 0.3)
    return {"x": x,
            "conv_w_words": conv_w_words,
            "conv_w_scales": conv_w_scales,
            "conv_b": conv_b,
            "conv_out_w_words": conv_out_w_words,
            "conv_out_w_scales": conv_out_w_scales,
            "conv_out_b": conv_out_b}


def reference(x, conv_w_words, conv_w_scales, conv_b, conv_out_w_words, conv_out_w_scales, conv_out_b):
    x = f64(x)
    b, l, c, h, w = x.shape
    pad_h = (2 - h % 2) % 2
    pad_w = (2 - w % 2) % 2
    if pad_h > 0 or pad_w > 0:
        x = np.pad(x, ((0, 0), (0, 0), (0, 0), (0, pad_h), (0, pad_w)))
    hp, wp = x.shape[-2], x.shape[-1]
    xf = x.reshape(b * l, c, hp, wp)
    x_dwt = _dwt(xf)
    n, c4, hh, wh = x_dwt.shape
    xq = mxq(x_dwt, 1, "e4m3").reshape(n, c4, hh * wh)
    feat = (unpack_weight(conv_w_words, conv_w_scales, FMT).T @ xq) + f64(conv_b)[None, :, None]
    feat = silu(feat)
    y = (unpack_weight(conv_out_w_words, conv_out_w_scales, FMT).T @ mxq(feat, 1, "e4m3")) + f64(conv_out_b)[None, :, None]
    rec = _idwt(y.reshape(n, c4, hh, wh))
    out = rec.reshape(b, l, c, hp, wp)
    if pad_h > 0 or pad_w > 0:
        out = out[..., :h, :w]
    return out

@@ -1,0 +1,301 @@
+from contextlib import ExitStack
+
+import concourse.mybir as mybir
+from concourse.masks import make_identity
+
+F32 = mybir.dt.float32
+BF16 = mybir.dt.bfloat16
+I32 = mybir.dt.int32
+U32 = mybir.dt.uint32
+U8 = mybir.dt.uint8
+FP8X4 = mybir.dt.float8_e4m3fn_x4
+ALU = mybir.AluOpType
+ACT = mybir.ActivationFunctionType
+
+P = 128
+FLOPS = 2 * 256 * 2048 * 4096 * 2
+
+
+def tile_waveletblock_w_kernel(tc, x, w1_words, w1_scales, b1, w2_words, w2_scales, b2, out):
+    nc = tc.nc
+    with ExitStack() as ctx:
+        ctx.enter_context(tc.manual_schedule())
+        keep = ctx.enter_context(tc.tile_pool(name="keep", bufs=1))
+        psum = ctx.enter_context(tc.psum_pool(name="psum", bufs=8))
+
+        w1 = keep.tile([P, 4, 4096], U32, align_bytes=64)
+        w2 = keep.tile([P, 8, 2048], U32, align_bytes=64)
+        w1s = keep.tile([P, 4096], U8, align_bytes=64)
+        w2s = keep.tile([P, 2, 2048], U8, align_bytes=64)
+        dq = keep.tile([P, 2, 4, 128], U32, align_bytes=64)
+        dsc = keep.tile([P, 2, 4, 128], U8, align_bytes=64)
+        fq = keep.tile([P, 8, 256], U32, align_bytes=64)
+        fsc = keep.tile([P, 8, 256], U8, align_bytes=64)
+        ident = keep.tile([P, P], BF16)
+        zt = keep.tile([P, 640], BF16)
+        bsrt = keep.tile([P, 8, 4, 128], BF16)
+        b2h = keep.tile([P, 16], F32)
+        bias_2s = keep.tile([P, 4], F32)
+        bias_2n = keep.tile([P, 4], F32)
+        bias_4p = keep.tile([P, 4], F32)
+        bias_4m = keep.tile([P, 4], F32)
+        warm_in = keep.tile([P, 1], F32)
+        warm_out = keep.tile([P, 1], F32)
+
+        w1_dram = w1_words.rearrange("g p n t -> p g (n t)")
+        w2_dram = w2_words.rearrange("g p n t -> p g (n t)")
+        x_dram = x.rearrange("b l (p t) h w -> p (b l) (t h w)", t=4)
+        out_dram = out.rearrange("b l (k c) h w -> k c (b l) (h w)", c=P)
+
+        with tc.tile_pool(name="head", bufs=1) as head:
+            x_sb = head.tile([P, 4, 4, 256], BF16)
+            gd = head.tile([P, 2, 4, 128, 4], BF16, align_bytes=64)
+
+            nc.vector.memset(zt[:], 0.0)
+            nc.vector.memset(warm_in[:], 0.0)
+            nc.vector.memset(w1s[:].bitcast(I32), 0)
+            nc.vector.memset(w2s[:].bitcast(I32), 0)
+            make_identity(nc, ident[:])
+
+            for tt in range(2):
+                nc.sync.dma_start(
+                    out=x_sb[:, 2 * tt : 2 * tt + 2].rearrange("p m t q -> p m (t q)"),
+                    in_=x_dram[:, 2 * tt : 2 * tt + 2, :],
+                )
+            nc.scalar.activation(out=warm_out[:], in_=warm_in[:], func=ACT.Silu)
+            nc.scalar.dma_start(out=zt[0:8, 0:512], in_=b1.rearrange("(r c) -> r c", c=512))
+            nc.scalar.dma_start(out=zt[0:16, 512:640], in_=b2.rearrange("(r c) -> r c", c=128))
+            for q in range(4):
+                nc.sync.dma_start(
+                    out=w1s[32 * q : 32 * q + 16, :].bitcast(I32),
+                    in_=w1_scales[:, 4 * q : 4 * q + 4, :].bitcast(I32),
+                )
+            for nt in range(8):
+                nc.sync.dma_start(
+                    out=w1[:, :, 512 * nt : 512 * (nt + 1)].bitcast(I32),
+                    in_=w1_dram[:, :, 2048 * nt : 2048 * (nt + 1)].bitcast(I32),
+                )
+            for h in range(2):
+                for q in range(4):
+                    nc.sync.dma_start(
+                        out=w2s[32 * q : 32 * q + 16, h, :].bitcast(I32),
+                        in_=w2_scales[4 * h : 4 * h + 4, 4 * q : 4 * q + 4, :].bitcast(I32),
+                    )
+            for s in (1, 2, 3, 0):
+                for h in range(2):
+                    nc.sync.dma_start(
+                        out=w2[:, 4 * h : 4 * h + 4, 512 * s : 512 * (s + 1)].bitcast(I32),
+                        in_=w2_dram[:, 4 * h : 4 * h + 4, 2048 * s : 2048 * (s + 1)].bitcast(I32),
+                    )
+
+            def bias_bcast(nt):
+                pb = psum.tile([P, 512], F32, tag="ps")
+                nc.tensor.matmul(
+                    out=pb[:],
+                    lhsT=ident[:, nt : nt + 1].to_broadcast([P, P]),
+                    rhs=zt[:, 0:512],
+                    start=True,
+                    stop=True,
+                )
+                nc.scalar.copy(out=bsrt[:, nt], in_=pb[:].rearrange("q (p t) -> q t p", t=4))
+
+            for nt in range(4):
+                bias_bcast(nt)
+            xb = x_sb[:, 2:4].rearrange("p m t q -> p (m t q)")
+            nc.scalar.mul(out=xb, in_=xb, mul=0.5)
+            for nt in range(4, 8):
+                bias_bcast(nt)
+
+            ptb = psum.tile([P, P], BF16, tag="ps")
+            nc.tensor.transpose(out=ptb[:], in_=zt[:, 512:640], identity=ident[:])
+            nc.scalar.activation(out=b2h[:], in_=ptb[:, 0:16], func=ACT.Copy, scale=0.5)
+            nc.gpsimd.tensor_tensor(out=bias_2s[:], in0=b2h[:, 8:12], in1=b2h[:, 4:8], op=ALU.add)
+            nc.gpsimd.tensor_tensor(out=bias_2n[:], in0=b2h[:, 8:12], in1=b2h[:, 4:8], op=ALU.subtract)
+            nc.gpsimd.tensor_tensor(out=bias_4p[:], in0=b2h[:, 0:4], in1=b2h[:, 12:16], op=ALU.add)
+            nc.gpsimd.tensor_tensor(out=bias_4m[:], in0=b2h[:, 0:4], in1=b2h[:, 12:16], op=ALU.subtract)
+
+            xa = x_sb[:, 0:2].rearrange("p m t q -> p (m t q)")
+            nc.vector.tensor_scalar_mul(out=xa, in0=xa, scalar1=0.5)
+
+            def dwt(tt):
+                s_t = head.tile([P, 2, 8, 16, 4], F32, tag="s", bufs=2)
+                e_t = head.tile([P, 2, 8, 16, 4], F32, tag="e", bufs=2)
+                for m in range(2):
+                    xv = x_sb[:, 2 * tt + m].rearrange("p t (i a r) -> p i a r t", a=2, r=16)
+                    nc.vector.tensor_tensor(out=s_t[:, m], in0=xv[:, :, 0], in1=xv[:, :, 1], op=ALU.add)
+                    nc.vector.tensor_tensor(out=e_t[:, m], in0=xv[:, :, 1], in1=xv[:, :, 0], op=ALU.subtract)
+                sv = s_t[:].rearrange("p m i (j b) t -> p (m i j) b t", b=2)
+                ev = e_t[:].rearrange("p m i (j b) t -> p (m i j) b t", b=2)
+                nc.vector.tensor_tensor(out=gd[:, tt, 0], in0=sv[:, :, 1], in1=sv[:, :, 0], op=ALU.add)
+                nc.vector.tensor_tensor(out=gd[:, tt, 1], in0=sv[:, :, 1], in1=sv[:, :, 0], op=ALU.subtract)
+                nc.vector.tensor_tensor(out=gd[:, tt, 2], in0=ev[:, :, 1], in1=ev[:, :, 0], op=ALU.add)
+                nc.vector.tensor_tensor(out=gd[:, tt, 3], in0=ev[:, :, 1], in1=ev[:, :, 0], op=ALU.subtract)
+                nc.vector.quantize_mx(
+                    out=dq[:, tt].rearrange("p g w -> p (g w)").bitcast(FP8X4),
+                    scales=dsc[:, tt].rearrange("p g w -> p (g w)"),
+                    in_=gd[:, tt].rearrange("p g w t -> p (g w t)"),
+                )
+
+            dwt(0)
+            dwt(1)
+
+        work = ctx.enter_context(tc.tile_pool(name="work", bufs=1))
+        fin = ctx.enter_context(tc.tile_pool(name="fin", bufs=1))
+
+        accs = {}
+        feats = {}
+        tps = {}
+        gfs = {}
+
+        def mm1(nt, tt):
+            acc = psum.tile([P, 512], F32, tag="ps")
+            for g in range(4):
+                nc.tensor.matmul_mx(
+                    out=acc[:],
+                    lhsT=dq[:, tt, g, :].bitcast(FP8X4),
+                    lhsT_scale=dsc[:, tt, g, :],
+                    rhs=w1[:, g, 512 * nt : 512 * (nt + 1)].bitcast(FP8X4),
+                    rhs_scale=w1s[4 * g : P, 512 * nt : 512 * (nt + 1)],
+                    start=(g == 0),
+                    stop=(g == 3),
+                )
+            accs[(nt, tt)] = acc
+
+        def ev1(nt, tt):
+            pre = work.tile([P, 4, 128], F32, tag="pre", bufs=4)
+            nc.vector.tensor_tensor(
+                out=pre[:],
+                in0=accs[(nt, tt)][:].rearrange("q (p t) -> q t p", t=4),
+                in1=bsrt[:, nt],
+                op=ALU.add,
+            )
+            fs = work.tile([P, 4, 128], BF16, tag="fs", bufs=8)
+            nc.scalar.activation(out=fs[:], in_=pre[:], func=ACT.Silu)
+            feats[(nt, tt)] = fs
+
+        def tr(nt):
+            for tt in range(2):
+                tp = psum.tile([P, 4, 128], BF16, tag="ps")
+                for t in range(4):
+                    nc.tensor.transpose(out=tp[:, t, :], in_=feats[(nt, tt)][:, t, :], identity=ident[:])
+                tps[(nt, tt)] = tp
+
+        def co(nt):
+            gf = work.tile([P, 256, 4], BF16, tag="gf", bufs=3, align_bytes=64)
+            nc.vector.tensor_copy(out=gf[:, 0:128, :], in_=tps[(nt, 0)][:].rearrange("p t w -> p w t"))
+            nc.scalar.copy(out=gf[:, 128:256, :], in_=tps[(nt, 1)][:].rearrange("p t w -> p w t"))
+            gfs[nt] = gf
+
+        def qf(nt):
+            nc.vector.quantize_mx(
+                out=fq[:, nt, :].bitcast(FP8X4),
+                scales=fsc[:, nt, :],
+                in_=gfs[nt][:].rearrange("p w t -> p (w t)"),
+            )
+
+        mm1(0, 0)
+        mm1(1, 0)
+        mm1(0, 1)
+        mm1(1, 1)
+        ev1(0, 0)
+        ev1(1, 0)
+        ev1(0, 1)
+        ev1(1, 1)
+        mm1(2, 0)
+        mm1(2, 1)
+        tr(0)
+        tr(1)
+        ev1(2, 0)
+        ev1(2, 1)
+        co(0)
+        co(1)
+        for nt in range(3, 8):
+            mm1(nt, 0)
+            mm1(nt, 1)
+            tr(nt - 1)
+            ev1(nt, 0)
+            qf(0 if nt == 3 else nt - 2)
+            ev1(nt, 1)
+            if nt == 3:
+                qf(1)
+            co(nt - 1)
+        qf(6)
+
+        def mm2(acc, s, ct, g):
+            m0 = 512 * s + 128 * ct
+            nc.tensor.matmul_mx(
+                out=acc[:],
+                lhsT=w2[:, g, m0 : m0 + 128].bitcast(FP8X4),
+                lhsT_scale=w2s[4 * (g % 4) : P, g // 4, m0 : m0 + 128],
+                rhs=fq[:, g, :].bitcast(FP8X4),
+                rhs_scale=fsc[:, g, :],
+                start=(g == 0),
+                stop=(g == 7),
+            )
+
+        y2s = fin.tile([P, 4, 256], F32)
+        y2n = fin.tile([P, 4, 256], F32)
+
+        first = []
+        for ct in range(4):
+            acc_a = psum.tile([P, 256], F32, tag="ps")
+            first.append(acc_a)
+        for g in range(3):
+            for ct in range(4):
+                mm2(first[ct], 1, ct, g)
+        tr(7)
+        co(7)
+        qf(7)
+        for g in range(3, 8):
+            for ct in range(4):
+                mm2(first[ct], 1, ct, g)
+        for ct in range(4):
+            nc.scalar.activation(
+                out=y2s[:, ct, :], in_=first[ct][:], func=ACT.Identity, bias=bias_2s[:, ct : ct + 1], scale=0.5
+            )
+            nc.scalar.activation(
+                out=y2n[:, ct, :], in_=first[ct][:], func=ACT.Identity, bias=bias_2n[:, ct : ct + 1], scale=-0.5
+            )
+
+        for ct in range(4):
+            acc_b = psum.tile([P, 256], F32, tag="ps")
+            for g in range(8):
+                mm2(acc_b, 2, ct, g)
+            nc.vector.scalar_tensor_tensor(
+                out=y2s[:, ct, :], in0=acc_b[:], scalar=0.5, in1=y2s[:, ct, :], op0=ALU.mult, op1=ALU.add
+            )
+            nc.vector.scalar_tensor_tensor(
+                out=y2n[:, ct, :], in0=acc_b[:], scalar=0.5, in1=y2n[:, ct, :], op0=ALU.mult, op1=ALU.add
+            )
+
+        planes = []
+        for ct in range(4):
+            acc_c = psum.tile([P, 256], F32, tag="ps")
+            for g in range(8):
+                mm2(acc_c, 3, ct, g)
+            y4p = fin.tile([P, 256], F32, tag="y4p", bufs=2)
+            y4m = fin.tile([P, 256], F32, tag="y4m", bufs=2)
+            nc.scalar.activation(out=y4p[:], in_=acc_c[:], func=ACT.Identity, bias=bias_4p[:, ct : ct + 1], scale=0.5)
+            nc.scalar.activation(out=y4m[:], in_=acc_c[:], func=ACT.Identity, bias=bias_4m[:, ct : ct + 1], scale=-0.5)
+            t_t = fin.tile([P, 4, 256], F32, tag="t", bufs=4)
+            nc.vector.tensor_tensor(out=t_t[:, 0, :], in0=y4p[:], in1=y2s[:, ct, :], op=ALU.subtract)
+            nc.vector.tensor_tensor(out=t_t[:, 1, :], in0=y4m[:], in1=y2n[:, ct, :], op=ALU.subtract)
+            nc.vector.tensor_tensor(out=t_t[:, 2, :], in0=y4m[:], in1=y2n[:, ct, :], op=ALU.add)
+            nc.vector.tensor_tensor(out=t_t[:, 3, :], in0=y4p[:], in1=y2s[:, ct, :], op=ALU.add)
+            planes.append(t_t)
+
+        for ct in range(4):
+            acc_d = psum.tile([P, 256], F32, tag="ps")
+            for g in range(8):
+                mm2(acc_d, 0, ct, g)
+            o_t = fin.tile([P, 4, 8, 2, 8, 2], F32, tag="o", bufs=3)
+            for a in range(2):
+                nc.vector.scalar_tensor_tensor(
+                    out=o_t[:, :, :, a].rearrange("p m i j b -> p (m i) j b"),
+                    in0=acc_d[:].rearrange("p (q j) -> p q j", j=8).unsqueeze(3).to_broadcast([P, 32, 8, 2]),
+                    scalar=0.5,
+                    in1=planes[ct][:, 2 * a : 2 * a + 2, :].rearrange("p b (q j) -> p q j b", j=8),
+                    op0=ALU.mult,
+                    op1=ALU.add,
+                )
+            nc.sync.dma_start(out=out_dram[ct], in_=o_t[:].rearrange("p m i a j b -> p m (i a j b)"))

@@ -31,159 +31,214 @@ def tile_waveletblock_w_kernel(tc, x, w1_words, w1_scales, b1, w2_words, w2_scal
         dsc = keep.tile([P, 2, 4, 128], U8, align_bytes=64)
         fq = keep.tile([P, 8, 256], U32, align_bytes=64)
         fsc = keep.tile([P, 8, 256], U8, align_bytes=64)
-        ident = keep.tile([P, P], BF16)
-        zt = keep.tile([P, 640], BF16)
-        bsrt = keep.tile([P, 8, 4, 128], BF16)
+        ident_b = keep.tile([P, P], BF16)
+        ident_f = keep.tile([P, P], F32)
+        half_p = keep.tile([P, P], BF16)
+        half_n = keep.tile([P, P], BF16)
+        zb2 = keep.tile([P, P], BF16)
+        b1raw = keep.tile([P, 8, 4], BF16)
+        b1t = keep.tile([P, 32], F32)
         b2h = keep.tile([P, 16], F32)
         bias_2s = keep.tile([P, 4], F32)
         bias_2n = keep.tile([P, 4], F32)
         bias_4p = keep.tile([P, 4], F32)
         bias_4m = keep.tile([P, 4], F32)
+        bias_e = keep.tile([P, 4], F32)
+        bias_f = keep.tile([P, 4], F32)
+        bias_p2 = keep.tile([P, 4], F32)
+        bias_m2 = keep.tile([P, 4], F32)
         warm_in = keep.tile([P, 1], F32)
         warm_out = keep.tile([P, 1], F32)
 
-        w1_dram = w1_words.rearrange("g p n t -> p g (n t)")
         w2_dram = w2_words.rearrange("g p n t -> p g (n t)")
         x_dram = x.rearrange("b l (p t) h w -> p (b l) (t h w)", t=4)
         out_dram = out.rearrange("b l (k c) h w -> k c (b l) (h w)", c=P)
 
         with tc.tile_pool(name="head", bufs=1) as head:
             x_sb = head.tile([P, 4, 4, 256], BF16)
+            xh = head.tile([P, 4, 4, 256], BF16)
             gd = head.tile([P, 2, 4, 128, 4], BF16, align_bytes=64)
 
-            nc.vector.memset(zt[:], 0.0)
+            nc.vector.memset(zb2[:], 0.0)
             nc.vector.memset(warm_in[:], 0.0)
             nc.vector.memset(w1s[:].bitcast(I32), 0)
             nc.vector.memset(w2s[:].bitcast(I32), 0)
-            make_identity(nc, ident[:])
+            make_identity(nc, ident_b[:])
+            make_identity(nc, ident_f[:])
+            nc.vector.tensor_scalar_mul(out=half_p[:], in0=ident_b[:], scalar1=0.5)
+            nc.vector.tensor_scalar_mul(out=half_n[:], in0=ident_b[:], scalar1=-0.5)
 
-            for tt in range(2):
-                nc.sync.dma_start(
-                    out=x_sb[:, 2 * tt : 2 * tt + 2].rearrange("p m t q -> p m (t q)"),
-                    in_=x_dram[:, 2 * tt : 2 * tt + 2, :],
-                )
+            for m in range(4):
+                nc.sync.dma_start(out=x_sb[:, m].rearrange("p t q -> p (t q)"), in_=x_dram[:, m, :])
+            nc.scalar.dma_start(out=b1raw[:], in_=b1.rearrange("(g p t) -> p g t", p=P, t=4))
+            nc.scalar.dma_start(out=zb2[0:16, :], in_=b2.rearrange("(r c) -> r c", c=128))
             nc.scalar.activation(out=warm_out[:], in_=warm_in[:], func=ACT.Silu)
-            nc.scalar.dma_start(out=zt[0:8, 0:512], in_=b1.rearrange("(r c) -> r c", c=512))
-            nc.scalar.dma_start(out=zt[0:16, 512:640], in_=b2.rearrange("(r c) -> r c", c=128))
             for q in range(4):
                 nc.sync.dma_start(
                     out=w1s[32 * q : 32 * q + 16, :].bitcast(I32),
                     in_=w1_scales[:, 4 * q : 4 * q + 4, :].bitcast(I32),
                 )
-            for nt in range(8):
-                nc.sync.dma_start(
-                    out=w1[:, :, 512 * nt : 512 * (nt + 1)].bitcast(I32),
-                    in_=w1_dram[:, :, 2048 * nt : 2048 * (nt + 1)].bitcast(I32),
-                )
+            for qd in range(4):
+                for g in range(4):
+                    nc.sync.dma_start(
+                        out=w1[:, g, 1024 * qd : 1024 * (qd + 1)].bitcast(I32),
+                        in_=w1_words[g].rearrange("p n t -> p (n t)")[:, 4096 * qd : 4096 * (qd + 1)].bitcast(I32),
+                    )
             for h in range(2):
                 for q in range(4):
                     nc.sync.dma_start(
                         out=w2s[32 * q : 32 * q + 16, h, :].bitcast(I32),
                         in_=w2_scales[4 * h : 4 * h + 4, 4 * q : 4 * q + 4, :].bitcast(I32),
                     )
-            for s in (1, 2, 3, 0):
+            for h in range(4):
+                nc.sync.dma_start(
+                    out=w2[:, 2 * h : 2 * h + 2, 512:1536].bitcast(I32),
+                    in_=w2_dram[:, 2 * h : 2 * h + 2, 2048:6144].bitcast(I32),
+                )
+            for s in (3, 0):
                 for h in range(2):
                     nc.sync.dma_start(
                         out=w2[:, 4 * h : 4 * h + 4, 512 * s : 512 * (s + 1)].bitcast(I32),
                         in_=w2_dram[:, 4 * h : 4 * h + 4, 2048 * s : 2048 * (s + 1)].bitcast(I32),
                     )
 
-            def bias_bcast(nt):
-                pb = psum.tile([P, 512], F32, tag="ps")
-                nc.tensor.matmul(
-                    out=pb[:],
-                    lhsT=ident[:, nt : nt + 1].to_broadcast([P, P]),
-                    rhs=zt[:, 0:512],
-                    start=True,
-                    stop=True,
+            nc.gpsimd.tensor_copy(out=b1t[:], in_=b1raw[:].rearrange("p g t -> p (g t)"))
+
+            def dwt_pe(tt):
+                xv = x_sb[:, 2 * tt : 2 * tt + 2].rearrange("p m t (i a j b) -> p a b (m t i) j", a=2, j=8, b=2)
+                for g in (2, 3):
+                    pd = psum.tile([P, 512], F32, tag="ps")
+                    n = 0
+                    for a in range(2):
+                        for b in range(2):
+                            plus = (a == 1) if g == 2 else (a == b)
+                            nc.tensor.matmul(
+                                out=pd[:].rearrange("p (c j) -> p c j", j=8),
+                                lhsT=(half_p if plus else half_n)[:],
+                                rhs=xv[:, a, b],
+                                start=(n == 0),
+                                stop=(n == 3),
+                            )
+                            n += 1
+                    nc.scalar.copy(
+                        out=gd[:, tt, g].rearrange("p (m q) t -> p m q t", m=2),
+                        in_=pd[:].rearrange("p (m t q) -> p m q t", m=2, t=4),
+                    )
+
+            sums = {}
+
+            def dwt_rows(m):
+                if m % 2 == 0:
+                    s_t = head.tile([P, 2, 8, 16, 4], F32, tag="s", bufs=2)
+                    sums[m // 2] = s_t
+                nc.vector.tensor_scalar_mul(
+                    out=xh[:, m].rearrange("p t q -> p (t q)"), in0=x_sb[:, m].rearrange("p t q -> p (t q)"), scalar1=0.5
                 )
-                nc.scalar.copy(out=bsrt[:, nt], in_=pb[:].rearrange("q (p t) -> q t p", t=4))
+                xv = xh[:, m].rearrange("p t (i a r) -> p i a r t", a=2, r=16)
+                nc.vector.tensor_tensor(out=sums[m // 2][:, m % 2], in0=xv[:, :, 0], in1=xv[:, :, 1], op=ALU.add)
 
-            for nt in range(4):
-                bias_bcast(nt)
-            xb = x_sb[:, 2:4].rearrange("p m t q -> p (m t q)")
-            nc.scalar.mul(out=xb, in_=xb, mul=0.5)
-            for nt in range(4, 8):
-                bias_bcast(nt)
-
-            ptb = psum.tile([P, P], BF16, tag="ps")
-            nc.tensor.transpose(out=ptb[:], in_=zt[:, 512:640], identity=ident[:])
-            nc.scalar.activation(out=b2h[:], in_=ptb[:, 0:16], func=ACT.Copy, scale=0.5)
-            nc.gpsimd.tensor_tensor(out=bias_2s[:], in0=b2h[:, 8:12], in1=b2h[:, 4:8], op=ALU.add)
-            nc.gpsimd.tensor_tensor(out=bias_2n[:], in0=b2h[:, 8:12], in1=b2h[:, 4:8], op=ALU.subtract)
-            nc.gpsimd.tensor_tensor(out=bias_4p[:], in0=b2h[:, 0:4], in1=b2h[:, 12:16], op=ALU.add)
-            nc.gpsimd.tensor_tensor(out=bias_4m[:], in0=b2h[:, 0:4], in1=b2h[:, 12:16], op=ALU.subtract)
-
-            xa = x_sb[:, 0:2].rearrange("p m t q -> p (m t q)")
-            nc.vector.tensor_scalar_mul(out=xa, in0=xa, scalar1=0.5)
-
-            def dwt(tt):
-                s_t = head.tile([P, 2, 8, 16, 4], F32, tag="s", bufs=2)
-                e_t = head.tile([P, 2, 8, 16, 4], F32, tag="e", bufs=2)
-                for m in range(2):
-                    xv = x_sb[:, 2 * tt + m].rearrange("p t (i a r) -> p i a r t", a=2, r=16)
-                    nc.vector.tensor_tensor(out=s_t[:, m], in0=xv[:, :, 0], in1=xv[:, :, 1], op=ALU.add)
-                    nc.vector.tensor_tensor(out=e_t[:, m], in0=xv[:, :, 1], in1=xv[:, :, 0], op=ALU.subtract)
-                sv = s_t[:].rearrange("p m i (j b) t -> p (m i j) b t", b=2)
-                ev = e_t[:].rearrange("p m i (j b) t -> p (m i j) b t", b=2)
+            def dwt_cols(tt):
+                sv = sums[tt][:].rearrange("p m i (j b) t -> p (m i j) b t", b=2)
                 nc.vector.tensor_tensor(out=gd[:, tt, 0], in0=sv[:, :, 1], in1=sv[:, :, 0], op=ALU.add)
                 nc.vector.tensor_tensor(out=gd[:, tt, 1], in0=sv[:, :, 1], in1=sv[:, :, 0], op=ALU.subtract)
-                nc.vector.tensor_tensor(out=gd[:, tt, 2], in0=ev[:, :, 1], in1=ev[:, :, 0], op=ALU.add)
-                nc.vector.tensor_tensor(out=gd[:, tt, 3], in0=ev[:, :, 1], in1=ev[:, :, 0], op=ALU.subtract)
+
+            def quant_d(tt):
                 nc.vector.quantize_mx(
                     out=dq[:, tt].rearrange("p g w -> p (g w)").bitcast(FP8X4),
                     scales=dsc[:, tt].rearrange("p g w -> p (g w)"),
                     in_=gd[:, tt].rearrange("p g w t -> p (g w t)"),
                 )
 
-            dwt(0)
-            dwt(1)
+            dwt_pe(0)
+            dwt_pe(1)
+            dwt_rows(0)
+            dwt_rows(1)
+            dwt_cols(0)
+            dwt_rows(2)
+            quant_d(0)
+            dwt_rows(3)
+            dwt_cols(1)
+            quant_d(1)
+
+            ptb = psum.tile([P, P], BF16, tag="ps")
+            nc.tensor.transpose(out=ptb[:], in_=zb2[:], identity=ident_b[:])
+            nc.scalar.activation(out=b2h[:], in_=ptb[:, 0:16], func=ACT.Copy, scale=0.5)
+            nc.gpsimd.tensor_tensor(out=bias_2s[:], in0=b2h[:, 8:12], in1=b2h[:, 4:8], op=ALU.add)
+            nc.gpsimd.tensor_tensor(out=bias_2n[:], in0=b2h[:, 8:12], in1=b2h[:, 4:8], op=ALU.subtract)
+            nc.gpsimd.tensor_tensor(out=bias_4p[:], in0=b2h[:, 0:4], in1=b2h[:, 12:16], op=ALU.add)
+            nc.gpsimd.tensor_tensor(out=bias_4m[:], in0=b2h[:, 0:4], in1=b2h[:, 12:16], op=ALU.subtract)
+            nc.gpsimd.tensor_tensor(out=bias_e[:], in0=bias_2s[:], in1=bias_4p[:], op=ALU.subtract)
+            nc.gpsimd.tensor_tensor(out=bias_f[:], in0=bias_2n[:], in1=bias_4m[:], op=ALU.subtract)
+            nc.gpsimd.tensor_tensor(out=bias_p2[:], in0=bias_4p[:], in1=bias_4p[:], op=ALU.add)
+            nc.gpsimd.tensor_tensor(out=bias_m2[:], in0=bias_4m[:], in1=bias_4m[:], op=ALU.add)
 
         work = ctx.enter_context(tc.tile_pool(name="work", bufs=1))
         fin = ctx.enter_context(tc.tile_pool(name="fin", bufs=1))
 
         accs = {}
-        feats = {}
+        pres = {}
         tps = {}
+        fpls = {}
         gfs = {}
 
-        def mm1(nt, tt):
-            acc = psum.tile([P, 512], F32, tag="ps")
-            for g in range(4):
-                nc.tensor.matmul_mx(
-                    out=acc[:],
-                    lhsT=dq[:, tt, g, :].bitcast(FP8X4),
-                    lhsT_scale=dsc[:, tt, g, :],
-                    rhs=w1[:, g, 512 * nt : 512 * (nt + 1)].bitcast(FP8X4),
-                    rhs_scale=w1s[4 * g : P, 512 * nt : 512 * (nt + 1)],
-                    start=(g == 0),
-                    stop=(g == 3),
-                )
-            accs[(nt, tt)] = acc
-
-        def ev1(nt, tt):
-            pre = work.tile([P, 4, 128], F32, tag="pre", bufs=4)
-            nc.vector.tensor_tensor(
-                out=pre[:],
-                in0=accs[(nt, tt)][:].rearrange("q (p t) -> q t p", t=4),
-                in1=bsrt[:, nt],
-                op=ALU.add,
+        def mm1_pass(nt, tt, g):
+            if g == 0:
+                acc = psum.tile([P, 512], F32, tag="ps")
+                accs[(nt, tt)] = acc
+            nc.tensor.matmul_mx(
+                out=accs[(nt, tt)][:],
+                lhsT=dq[:, tt, g, :].bitcast(FP8X4),
+                lhsT_scale=dsc[:, tt, g, :],
+                rhs=w1[:, g, 512 * nt : 512 * (nt + 1)].bitcast(FP8X4),
+                rhs_scale=w1s[4 * g : P, 512 * nt : 512 * (nt + 1)],
+                start=(g == 0),
+                stop=(g == 3),
             )
-            fs = work.tile([P, 4, 128], BF16, tag="fs", bufs=8)
-            nc.scalar.activation(out=fs[:], in_=pre[:], func=ACT.Silu)
-            feats[(nt, tt)] = fs
+
+        def mm1(nt):
+            for tt in range(2):
+                for g in range(4):
+                    mm1_pass(nt, tt, g)
+
+        def cp(nt):
+            for tt in range(2):
+                pre = work.tile([P, 4, 128], F32, tag="pre", bufs=8)
+                src = accs[(nt, tt)][:].rearrange("q (p t) -> q t p", t=4)
+                if tt == 0:
+                    nc.vector.tensor_copy(out=pre[:], in_=src)
+                else:
+                    nc.scalar.copy(out=pre[:], in_=src)
+                pres[(nt, tt)] = pre
 
         def tr(nt):
-            for tt in range(2):
-                tp = psum.tile([P, 4, 128], BF16, tag="ps")
-                for t in range(4):
-                    nc.tensor.transpose(out=tp[:, t, :], in_=feats[(nt, tt)][:, t, :], identity=ident[:])
-                tps[(nt, tt)] = tp
+            for tp2 in range(2):
+                tpf = psum.tile([P, 2, 256], F32, tag="ps")
+                for t2 in range(2):
+                    for tt in range(2):
+                        nc.tensor.transpose(
+                            out=tpf[:, t2, 128 * tt : 128 * (tt + 1)],
+                            in_=pres[(nt, tt)][:, 2 * tp2 + t2, :],
+                            identity=ident_f[:],
+                        )
+                tps[(nt, tp2)] = tpf
 
-        def co(nt):
-            gf = work.tile([P, 256, 4], BF16, tag="gf", bufs=3, align_bytes=64)
-            nc.vector.tensor_copy(out=gf[:, 0:128, :], in_=tps[(nt, 0)][:].rearrange("p t w -> p w t"))
-            nc.scalar.copy(out=gf[:, 128:256, :], in_=tps[(nt, 1)][:].rearrange("p t w -> p w t"))
+        def si(nt):
+            fpl = work.tile([P, 4, 256], BF16, tag="fpl", bufs=4)
+            for t in range(4):
+                nc.scalar.activation(
+                    out=fpl[:, t, :],
+                    in_=tps[(nt, t // 2)][:, t % 2, :],
+                    func=ACT.Silu,
+                    bias=b1t[:, 4 * nt + t : 4 * nt + t + 1],
+                )
+            fpls[nt] = fpl
+
+        def rg(nt):
+            gf = work.tile([P, 256, 4], BF16, tag="gf", bufs=4, align_bytes=64)
+            nc.vector.tensor_copy(
+                out=gf[:].rearrange("p (c i) t -> p c t i", i=4),
+                in_=fpls[nt][:].rearrange("p t (c i) -> p c t i", i=4),
+            )
             gfs[nt] = gf
 
         def qf(nt):
@@ -193,33 +248,59 @@ def tile_waveletblock_w_kernel(tc, x, w1_words, w1_scales, b1, w2_words, w2_scal
                 in_=gfs[nt][:].rearrange("p w t -> p (w t)"),
             )
 
-        mm1(0, 0)
-        mm1(1, 0)
-        mm1(0, 1)
-        mm1(1, 1)
-        ev1(0, 0)
-        ev1(1, 0)
-        ev1(0, 1)
-        ev1(1, 1)
-        mm1(2, 0)
-        mm1(2, 1)
+        for g in range(3):
+            for nt in range(2):
+                mm1_pass(nt, 0, g)
+        for g in range(3):
+            for nt in range(2):
+                mm1_pass(nt, 1, g)
+        for tt in range(2):
+            for nt in range(2):
+                mm1_pass(nt, tt, 3)
+        cp(0)
+        cp(1)
+        for g in range(2):
+            for nt in (2, 3):
+                for tt in range(2):
+                    mm1_pass(nt, tt, g)
         tr(0)
         tr(1)
-        ev1(2, 0)
-        ev1(2, 1)
-        co(0)
-        co(1)
-        for nt in range(3, 8):
-            mm1(nt, 0)
-            mm1(nt, 1)
-            tr(nt - 1)
-            ev1(nt, 0)
-            qf(0 if nt == 3 else nt - 2)
-            ev1(nt, 1)
-            if nt == 3:
-                qf(1)
-            co(nt - 1)
-        qf(6)
+        si(0)
+        si(1)
+        for g in (2, 3):
+            for nt in (2, 3):
+                for tt in range(2):
+                    mm1_pass(nt, tt, g)
+        cp(2)
+        cp(3)
+        rg(0)
+        rg(1)
+        qf(0)
+        qf(1)
+        mm1(4)
+        cp(4)
+        tr(2)
+        tr(3)
+        si(2)
+        si(3)
+        mm1(5)
+        cp(5)
+        rg(2)
+        rg(3)
+        qf(2)
+        qf(3)
+        mm1(6)
+        cp(6)
+        tr(4)
+        tr(5)
+        si(4)
+        si(5)
+        mm1(7)
+        cp(7)
+        rg(4)
+        rg(5)
+        qf(4)
+        qf(5)
 
         def mm2(acc, s, ct, g):
             m0 = 512 * s + 128 * ct
@@ -240,27 +321,46 @@ def tile_waveletblock_w_kernel(tc, x, w1_words, w1_scales, b1, w2_words, w2_scal
         for ct in range(4):
             acc_a = psum.tile([P, 256], F32, tag="ps")
             first.append(acc_a)
-        for g in range(3):
+        for g in range(2):
             for ct in range(4):
                 mm2(first[ct], 1, ct, g)
+        tr(6)
         tr(7)
-        co(7)
+        si(6)
+        si(7)
+        rg(6)
+        rg(7)
+        qf(6)
         qf(7)
-        for g in range(3, 8):
+        for g in range(2, 6):
             for ct in range(4):
                 mm2(first[ct], 1, ct, g)
+        second = []
+        for ct in range(2):
+            acc_b = psum.tile([P, 256], F32, tag="ps")
+            second.append(acc_b)
+            for g in range(6):
+                mm2(acc_b, 2, ct, g)
+        for g in range(6, 8):
+            for ct in range(4):
+                mm2(first[ct], 1, ct, g)
+            for ct in range(2):
+                mm2(second[ct], 2, ct, g)
         for ct in range(4):
             nc.scalar.activation(
-                out=y2s[:, ct, :], in_=first[ct][:], func=ACT.Identity, bias=bias_2s[:, ct : ct + 1], scale=0.5
+                out=y2s[:, ct, :], in_=first[ct][:], func=ACT.Identity, bias=bias_e[:, ct : ct + 1], scale=0.5
             )
             nc.scalar.activation(
-                out=y2n[:, ct, :], in_=first[ct][:], func=ACT.Identity, bias=bias_2n[:, ct : ct + 1], scale=-0.5
+                out=y2n[:, ct, :], in_=first[ct][:], func=ACT.Identity, bias=bias_f[:, ct : ct + 1], scale=-0.5
             )
 
         for ct in range(4):
-            acc_b = psum.tile([P, 256], F32, tag="ps")
-            for g in range(8):
-                mm2(acc_b, 2, ct, g)
+            if ct < 2:
+                acc_b = second[ct]
+            else:
+                acc_b = psum.tile([P, 256], F32, tag="ps")
+                for g in range(8):
+                    mm2(acc_b, 2, ct, g)
             nc.vector.scalar_tensor_tensor(
                 out=y2s[:, ct, :], in0=acc_b[:], scalar=0.5, in1=y2s[:, ct, :], op0=ALU.mult, op1=ALU.add
             )
@@ -275,13 +375,17 @@ def tile_waveletblock_w_kernel(tc, x, w1_words, w1_scales, b1, w2_words, w2_scal
                 mm2(acc_c, 3, ct, g)
             y4p = fin.tile([P, 256], F32, tag="y4p", bufs=2)
             y4m = fin.tile([P, 256], F32, tag="y4m", bufs=2)
-            nc.scalar.activation(out=y4p[:], in_=acc_c[:], func=ACT.Identity, bias=bias_4p[:, ct : ct + 1], scale=0.5)
-            nc.scalar.activation(out=y4m[:], in_=acc_c[:], func=ACT.Identity, bias=bias_4m[:, ct : ct + 1], scale=-0.5)
+            nc.scalar.activation(out=y4p[:], in_=acc_c[:], func=ACT.Identity, bias=bias_p2[:, ct : ct + 1], scale=0.5)
+            nc.scalar.activation(out=y4m[:], in_=acc_c[:], func=ACT.Identity, bias=bias_m2[:, ct : ct + 1], scale=-0.5)
             t_t = fin.tile([P, 4, 256], F32, tag="t", bufs=4)
-            nc.vector.tensor_tensor(out=t_t[:, 0, :], in0=y4p[:], in1=y2s[:, ct, :], op=ALU.subtract)
-            nc.vector.tensor_tensor(out=t_t[:, 1, :], in0=y4m[:], in1=y2n[:, ct, :], op=ALU.subtract)
-            nc.vector.tensor_tensor(out=t_t[:, 2, :], in0=y4m[:], in1=y2n[:, ct, :], op=ALU.add)
-            nc.vector.tensor_tensor(out=t_t[:, 3, :], in0=y4p[:], in1=y2s[:, ct, :], op=ALU.add)
+            nc.vector.scalar_tensor_tensor(
+                out=t_t[:, 0, :], in0=acc_c[:], scalar=0.5, in1=y2s[:, ct, :], op0=ALU.mult, op1=ALU.subtract
+            )
+            nc.vector.scalar_tensor_tensor(
+                out=t_t[:, 1, :], in0=acc_c[:], scalar=-0.5, in1=y2n[:, ct, :], op0=ALU.mult, op1=ALU.subtract
+            )
+            nc.gpsimd.tensor_tensor(out=t_t[:, 2, :], in0=y4m[:], in1=y2n[:, ct, :], op=ALU.add)
+            nc.gpsimd.tensor_tensor(out=t_t[:, 3, :], in0=y4p[:], in1=y2s[:, ct, :], op=ALU.add)
             planes.append(t_t)
 
         for ct in range(4):

@@ -95,12 +95,16 @@ def tile_waveletblock_w_kernel(tc, x, w1_words, w1_scales, b1, w2_words, w2_scal
                     out=w2[:, 2 * h : 2 * h + 2, 512:1536].bitcast(I32),
                     in_=w2_dram[:, 2 * h : 2 * h + 2, 2048:6144].bitcast(I32),
                 )
-            for s in (3, 0):
-                for h in range(2):
-                    nc.sync.dma_start(
-                        out=w2[:, 4 * h : 4 * h + 4, 512 * s : 512 * (s + 1)].bitcast(I32),
-                        in_=w2_dram[:, 4 * h : 4 * h + 4, 2048 * s : 2048 * (s + 1)].bitcast(I32),
-                    )
+            for h in range(2):
+                nc.sync.dma_start(
+                    out=w2[:, 4 * h : 4 * h + 4, 1536:2048].bitcast(I32),
+                    in_=w2_dram[:, 4 * h : 4 * h + 4, 6144:8192].bitcast(I32),
+                )
+            for h in range(2):
+                nc.sync.dma_start(
+                    out=w2[:, :, 256 * h : 256 * (h + 1)].bitcast(I32),
+                    in_=w2_dram[:, :, 1024 * h : 1024 * (h + 1)].bitcast(I32),
+                )
 
             nc.gpsimd.tensor_copy(out=b1t[:], in_=b1raw[:].rearrange("p g t -> p (g t)"))
 
@@ -368,8 +372,9 @@ def tile_waveletblock_w_kernel(tc, x, w1_words, w1_scales, b1, w2_words, w2_scal
                 out=y2n[:, ct, :], in0=acc_b[:], scalar=0.5, in1=y2n[:, ct, :], op0=ALU.mult, op1=ALU.add
             )
 
-        planes = []
-        for ct in range(4):
+        planes = {}
+
+        def third(ct):
             acc_c = psum.tile([P, 256], F32, tag="ps")
             for g in range(8):
                 mm2(acc_c, 3, ct, g)
@@ -386,9 +391,9 @@ def tile_waveletblock_w_kernel(tc, x, w1_words, w1_scales, b1, w2_words, w2_scal
             )
             nc.gpsimd.tensor_tensor(out=t_t[:, 2, :], in0=y4m[:], in1=y2n[:, ct, :], op=ALU.add)
             nc.gpsimd.tensor_tensor(out=t_t[:, 3, :], in0=y4p[:], in1=y2s[:, ct, :], op=ALU.add)
-            planes.append(t_t)
+            planes[ct] = t_t
 
-        for ct in range(4):
+        def last(ct):
             acc_d = psum.tile([P, 256], F32, tag="ps")
             for g in range(8):
                 mm2(acc_d, 0, ct, g)
@@ -403,3 +408,9 @@ def tile_waveletblock_w_kernel(tc, x, w1_words, w1_scales, b1, w2_words, w2_scal
                     op1=ALU.add,
                 )
             nc.sync.dma_start(out=out_dram[ct], in_=o_t[:].rearrange("p m i a j b -> p m (i a j b)"))
+
+        for pair in range(2):
+            third(2 * pair)
+            third(2 * pair + 1)
+            last(2 * pair)
+            last(2 * pair + 1)

@@ -47,6 +47,7 @@ def tile_waveletblock_w_kernel(tc, x, w1_words, w1_scales, b1, w2_words, w2_scal
         bias_f = keep.tile([P, 4], F32)
         bias_p2 = keep.tile([P, 4], F32)
         bias_m2 = keep.tile([P, 4], F32)
+        wz = keep.tile([P, 512], BF16)
         warm_in = keep.tile([P, 1], F32)
         warm_out = keep.tile([P, 1], F32)
 
@@ -59,6 +60,7 @@ def tile_waveletblock_w_kernel(tc, x, w1_words, w1_scales, b1, w2_words, w2_scal
             xh = head.tile([P, 4, 4, 256], BF16)
             gd = head.tile([P, 2, 4, 128, 4], BF16, align_bytes=64)
 
+            nc.vector.memset(wz[:], 0.0)
             nc.vector.memset(zb2[:], 0.0)
             nc.vector.memset(warm_in[:], 0.0)
             nc.vector.memset(w1s[:].bitcast(I32), 0)
@@ -73,12 +75,14 @@ def tile_waveletblock_w_kernel(tc, x, w1_words, w1_scales, b1, w2_words, w2_scal
             nc.scalar.dma_start(out=b1raw[:], in_=b1.rearrange("(g p t) -> p g t", p=P, t=4))
             nc.scalar.dma_start(out=zb2[0:16, :], in_=b2.rearrange("(r c) -> r c", c=128))
             nc.scalar.activation(out=warm_out[:], in_=warm_in[:], func=ACT.Silu)
-            for q in range(4):
-                nc.sync.dma_start(
-                    out=w1s[32 * q : 32 * q + 16, :].bitcast(I32),
-                    in_=w1_scales[:, 4 * q : 4 * q + 4, :].bitcast(I32),
-                )
             for qd in range(4):
+                if qd < 2:
+                    c0, c1 = (0, 1024) if qd == 0 else (1024, 4096)
+                    for q in range(4):
+                        nc.sync.dma_start(
+                            out=w1s[32 * q : 32 * q + 16, c0:c1].bitcast(I32),
+                            in_=w1_scales[:, 4 * q : 4 * q + 4, c0:c1].bitcast(I32),
+                        )
                 for g in range(4):
                     nc.sync.dma_start(
                         out=w1[:, g, 1024 * qd : 1024 * (qd + 1)].bitcast(I32),
@@ -153,6 +157,9 @@ def tile_waveletblock_w_kernel(tc, x, w1_words, w1_scales, b1, w2_words, w2_scal
                     in_=gd[:, tt].rearrange("p g w t -> p (g w t)"),
                 )
 
+            pw = psum.tile([P, 512], F32, tag="ps")
+            for n in range(8):
+                nc.tensor.matmul(out=pw[:], lhsT=wz[:, 0:P], rhs=wz[:], start=True, stop=True)
             dwt_pe(0)
             dwt_pe(1)
             dwt_rows(0)
@@ -281,13 +288,19 @@ def tile_waveletblock_w_kernel(tc, x, w1_words, w1_scales, b1, w2_words, w2_scal
         rg(1)
         qf(0)
         qf(1)
-        mm1(4)
-        cp(4)
+        for g in range(2):
+            for nt in (4, 5):
+                for tt in range(2):
+                    mm1_pass(nt, tt, g)
         tr(2)
         tr(3)
         si(2)
         si(3)
-        mm1(5)
+        for g in (2, 3):
+            for nt in (4, 5):
+                for tt in range(2):
+                    mm1_pass(nt, tt, g)
+        cp(4)
         cp(5)
         rg(2)
         rg(3)
@@ -333,8 +346,8 @@ def tile_waveletblock_w_kernel(tc, x, w1_words, w1_scales, b1, w2_words, w2_scal
         si(6)
         si(7)
         rg(6)
-        rg(7)
         qf(6)
+        rg(7)
         qf(7)
         for g in range(2, 6):
             for ct in range(4):

@@ -35,8 +35,8 @@ def tile_waveletblock_w_kernel(tc, x, w1_words, w1_scales, b1, w2_words, w2_scal
         ident_f = keep.tile([P, P], F32)
         half_p = keep.tile([P, P], BF16)
         half_n = keep.tile([P, P], BF16)
-        zb2 = keep.tile([P, P], BF16)
-        b1raw = keep.tile([P, 8, 4], BF16)
+        bz = keep.tile([P, 640], BF16)
+        bs = keep.tile([P, 4, 128], BF16)
         b1t = keep.tile([P, 32], F32)
         b2h = keep.tile([P, 16], F32)
         bias_2s = keep.tile([P, 4], F32)
@@ -61,7 +61,7 @@ def tile_waveletblock_w_kernel(tc, x, w1_words, w1_scales, b1, w2_words, w2_scal
             gd = head.tile([P, 2, 4, 128, 4], BF16, align_bytes=64)
 
             nc.vector.memset(wz[:], 0.0)
-            nc.vector.memset(zb2[:], 0.0)
+            nc.vector.memset(bz[:], 0.0)
             nc.vector.memset(warm_in[:], 0.0)
             nc.vector.memset(w1s[:].bitcast(I32), 0)
             nc.vector.memset(w2s[:].bitcast(I32), 0)
@@ -72,27 +72,32 @@ def tile_waveletblock_w_kernel(tc, x, w1_words, w1_scales, b1, w2_words, w2_scal
 
             for m in range(4):
                 nc.sync.dma_start(out=x_sb[:, m].rearrange("p t q -> p (t q)"), in_=x_dram[:, m, :])
-            nc.scalar.dma_start(out=b1raw[:], in_=b1.rearrange("(g p t) -> p g t", p=P, t=4))
-            nc.scalar.dma_start(out=zb2[0:16, :], in_=b2.rearrange("(r c) -> r c", c=128))
+            nc.scalar.dma_start(out=bz[0:8, 0:512], in_=b1.rearrange("(r c) -> r c", c=512))
+            nc.scalar.dma_start(out=bz[0:16, 512:640], in_=b2.rearrange("(r c) -> r c", c=128))
             nc.scalar.activation(out=warm_out[:], in_=warm_in[:], func=ACT.Silu)
+            nc.scalar.copy(out=bs[:], in_=bz[:, 0:512].rearrange("k (p t) -> k t p", t=4))
+            for q in range(4):
+                nc.gpsimd.dma_start(
+                    out=w1s[32 * q : 32 * q + 16, 1024:4096].bitcast(F32),
+                    in_=w1_scales[:, 4 * q : 4 * q + 4, 1024:4096].bitcast(F32),
+                )
+            for h in range(2):
+                for q in range(4):
+                    nc.gpsimd.dma_start(
+                        out=w2s[32 * q : 32 * q + 16, h, :].bitcast(F32),
+                        in_=w2_scales[4 * h : 4 * h + 4, 4 * q : 4 * q + 4, :].bitcast(F32),
+                    )
             for qd in range(4):
-                if qd < 2:
-                    c0, c1 = (0, 1024) if qd == 0 else (1024, 4096)
+                if qd == 0:
                     for q in range(4):
                         nc.sync.dma_start(
-                            out=w1s[32 * q : 32 * q + 16, c0:c1].bitcast(I32),
-                            in_=w1_scales[:, 4 * q : 4 * q + 4, c0:c1].bitcast(I32),
+                            out=w1s[32 * q : 32 * q + 16, 0:1024].bitcast(I32),
+                            in_=w1_scales[:, 4 * q : 4 * q + 4, 0:1024].bitcast(I32),
                         )
                 for g in range(4):
                     nc.sync.dma_start(
                         out=w1[:, g, 1024 * qd : 1024 * (qd + 1)].bitcast(I32),
                         in_=w1_words[g].rearrange("p n t -> p (n t)")[:, 4096 * qd : 4096 * (qd + 1)].bitcast(I32),
-                    )
-            for h in range(2):
-                for q in range(4):
-                    nc.sync.dma_start(
-                        out=w2s[32 * q : 32 * q + 16, h, :].bitcast(I32),
-                        in_=w2_scales[4 * h : 4 * h + 4, 4 * q : 4 * q + 4, :].bitcast(I32),
                     )
             for h in range(4):
                 nc.sync.dma_start(
@@ -109,8 +114,6 @@ def tile_waveletblock_w_kernel(tc, x, w1_words, w1_scales, b1, w2_words, w2_scal
                     out=w2[:, :, 256 * h : 256 * (h + 1)].bitcast(I32),
                     in_=w2_dram[:, :, 1024 * h : 1024 * (h + 1)].bitcast(I32),
                 )
-
-            nc.gpsimd.tensor_copy(out=b1t[:], in_=b1raw[:].rearrange("p g t -> p (g t)"))
 
             def dwt_pe(tt):
                 xv = x_sb[:, 2 * tt : 2 * tt + 2].rearrange("p m t (i a j b) -> p a b (m t i) j", a=2, j=8, b=2)
@@ -171,9 +174,14 @@ def tile_waveletblock_w_kernel(tc, x, w1_words, w1_scales, b1, w2_words, w2_scal
             dwt_cols(1)
             quant_d(1)
 
-            ptb = psum.tile([P, P], BF16, tag="ps")
-            nc.tensor.transpose(out=ptb[:], in_=zb2[:], identity=ident_b[:])
-            nc.scalar.activation(out=b2h[:], in_=ptb[:, 0:16], func=ACT.Copy, scale=0.5)
+            ptb = psum.tile([P, 5, 128], BF16, tag="ps")
+            for t in range(4):
+                nc.tensor.transpose(out=ptb[:, t, :], in_=bs[:, t, :], identity=ident_b[:])
+            nc.tensor.transpose(out=ptb[:, 4, :], in_=bz[:, 512:640], identity=ident_b[:])
+            nc.scalar.copy(
+                out=b1t[:].rearrange("p (g t) -> p g t", t=4), in_=ptb[:, 0:4, 0:8].rearrange("p t g -> p g t")
+            )
+            nc.scalar.activation(out=b2h[:], in_=ptb[:, 4, 0:16], func=ACT.Copy, scale=0.5)
             nc.gpsimd.tensor_tensor(out=bias_2s[:], in0=b2h[:, 8:12], in1=b2h[:, 4:8], op=ALU.add)
             nc.gpsimd.tensor_tensor(out=bias_2n[:], in0=b2h[:, 8:12], in1=b2h[:, 4:8], op=ALU.subtract)
             nc.gpsimd.tensor_tensor(out=bias_4p[:], in0=b2h[:, 0:4], in1=b2h[:, 12:16], op=ALU.add)

@@ -21,22 +21,23 @@ def tile_waveletblock_w_kernel(tc, x, w1_words, w1_scales, b1, w2_words, w2_scal
     with ExitStack() as ctx:
         ctx.enter_context(tc.manual_schedule())
         keep = ctx.enter_context(tc.tile_pool(name="keep", bufs=1))
+        work = ctx.enter_context(tc.tile_pool(name="work", bufs=1))
         psum = ctx.enter_context(tc.psum_pool(name="psum", bufs=8))
 
-        w1 = keep.tile([P, 4, 4096], U32, align_bytes=64)
+        w1p = keep.tile([P, 8, 4, 512], U32, align_bytes=64)
         w2 = keep.tile([P, 8, 2048], U32, align_bytes=64)
         w1s = keep.tile([P, 4096], U8, align_bytes=64)
+        w1sp = keep.tile([P, 4096], U8, align_bytes=64)
         w2s = keep.tile([P, 2, 2048], U8, align_bytes=64)
-        dq = keep.tile([P, 2, 4, 128], U32, align_bytes=64)
-        dsc = keep.tile([P, 2, 4, 128], U8, align_bytes=64)
+        dq = keep.tile([P, 4, 256], U32, align_bytes=64)
+        dsc = keep.tile([P, 4, 256], U8, align_bytes=64)
         fq = keep.tile([P, 8, 256], U32, align_bytes=64)
         fsc = keep.tile([P, 8, 256], U8, align_bytes=64)
-        ident_b = keep.tile([P, P], BF16)
-        ident_f = keep.tile([P, P], F32)
-        half_p = keep.tile([P, P], BF16)
-        half_n = keep.tile([P, P], BF16)
+        ident = keep.tile([P, P], BF16)
+        half_i = keep.tile([P, P], BF16)
+        rows_sd = keep.tile([P, 2, 64], BF16)
+        haar = keep.tile([P, 4, 32], BF16)
         bz = keep.tile([P, 640], BF16)
-        bs = keep.tile([P, 4, 128], BF16)
         b1t = keep.tile([P, 32], F32)
         b2h = keep.tile([P, 16], F32)
         bias_2s = keep.tile([P, 4], F32)
@@ -51,133 +52,230 @@ def tile_waveletblock_w_kernel(tc, x, w1_words, w1_scales, b1, w2_words, w2_scal
         warm_in = keep.tile([P, 1], F32)
         warm_out = keep.tile([P, 1], F32)
 
+        w1_dram = w1_words.rearrange("g p n t -> p g (n t)")
         w2_dram = w2_words.rearrange("g p n t -> p g (n t)")
         x_dram = x.rearrange("b l (p t) h w -> p (b l) (t h w)", t=4)
         out_dram = out.rearrange("b l (k c) h w -> k c (b l) (h w)", c=P)
 
+        accs = {}
+        fpls = {}
+        gfs = {}
+
         with tc.tile_pool(name="head", bufs=1) as head:
             x_sb = head.tile([P, 4, 4, 256], BF16)
-            xh = head.tile([P, 4, 4, 256], BF16)
-            gd = head.tile([P, 2, 4, 128, 4], BF16, align_bytes=64)
+            x_t = head.tile([P, 8, 4, 128], BF16)
+            gd = head.tile([P, 4, 256, 4], BF16, align_bytes=64)
 
-            nc.vector.memset(wz[:], 0.0)
-            nc.vector.memset(bz[:], 0.0)
             nc.vector.memset(warm_in[:], 0.0)
+            nc.vector.memset(wz[:], 0.0)
             nc.vector.memset(w1s[:].bitcast(I32), 0)
-            nc.vector.memset(w2s[:].bitcast(I32), 0)
-            make_identity(nc, ident_b[:])
-            make_identity(nc, ident_f[:])
-            nc.vector.tensor_scalar_mul(out=half_p[:], in0=ident_b[:], scalar1=0.5)
-            nc.vector.tensor_scalar_mul(out=half_n[:], in0=ident_b[:], scalar1=-0.5)
+            nc.vector.memset(bz[:], 0.0)
+            make_identity(nc, ident[:])
 
             for m in range(4):
                 nc.sync.dma_start(out=x_sb[:, m].rearrange("p t q -> p (t q)"), in_=x_dram[:, m, :])
+            nc.scalar.activation(out=warm_out[:], in_=warm_in[:], func=ACT.Silu)
             nc.scalar.dma_start(out=bz[0:8, 0:512], in_=b1.rearrange("(r c) -> r c", c=512))
             nc.scalar.dma_start(out=bz[0:16, 512:640], in_=b2.rearrange("(r c) -> r c", c=128))
-            nc.scalar.activation(out=warm_out[:], in_=warm_in[:], func=ACT.Silu)
-            nc.scalar.copy(out=bs[:], in_=bz[:, 0:512].rearrange("k (p t) -> k t p", t=4))
             for q in range(4):
                 nc.gpsimd.dma_start(
                     out=w1s[32 * q : 32 * q + 16, 1024:4096].bitcast(F32),
                     in_=w1_scales[:, 4 * q : 4 * q + 4, 1024:4096].bitcast(F32),
                 )
+            nc.vector.memset(w2s[:].bitcast(I32), 0)
             for h in range(2):
                 for q in range(4):
                     nc.gpsimd.dma_start(
                         out=w2s[32 * q : 32 * q + 16, h, :].bitcast(F32),
                         in_=w2_scales[4 * h : 4 * h + 4, 4 * q : 4 * q + 4, :].bitcast(F32),
                     )
-            for qd in range(4):
-                if qd == 0:
-                    for q in range(4):
-                        nc.sync.dma_start(
-                            out=w1s[32 * q : 32 * q + 16, 0:1024].bitcast(I32),
-                            in_=w1_scales[:, 4 * q : 4 * q + 4, 0:1024].bitcast(I32),
-                        )
-                for g in range(4):
+            for q in range(4):
+                nc.sync.dma_start(
+                    out=w1s[32 * q : 32 * q + 16, 0:1024].bitcast(I32),
+                    in_=w1_scales[:, 4 * q : 4 * q + 4, 0:1024].bitcast(I32),
+                )
+            raws = {}
+
+            def load_w1(gg):
+                raw = head.tile([P, 4, 512], U32, tag="raw", bufs=4, align_bytes=64)
+                raws[gg] = raw
+                step = 1 if gg == 0 else 4
+                for g in range(0, 4, step):
                     nc.sync.dma_start(
-                        out=w1[:, g, 1024 * qd : 1024 * (qd + 1)].bitcast(I32),
-                        in_=w1_words[g].rearrange("p n t -> p (n t)")[:, 4096 * qd : 4096 * (qd + 1)].bitcast(I32),
-                    )
-            for h in range(4):
-                nc.sync.dma_start(
-                    out=w2[:, 2 * h : 2 * h + 2, 512:1536].bitcast(I32),
-                    in_=w2_dram[:, 2 * h : 2 * h + 2, 2048:6144].bitcast(I32),
-                )
-            for h in range(2):
-                nc.sync.dma_start(
-                    out=w2[:, 4 * h : 4 * h + 4, 1536:2048].bitcast(I32),
-                    in_=w2_dram[:, 4 * h : 4 * h + 4, 6144:8192].bitcast(I32),
-                )
-            for h in range(2):
-                nc.sync.dma_start(
-                    out=w2[:, :, 256 * h : 256 * (h + 1)].bitcast(I32),
-                    in_=w2_dram[:, :, 1024 * h : 1024 * (h + 1)].bitcast(I32),
-                )
-
-            def dwt_pe(tt):
-                xv = x_sb[:, 2 * tt : 2 * tt + 2].rearrange("p m t (i a j b) -> p a b (m t i) j", a=2, j=8, b=2)
-                for g in (2, 3):
-                    pd = psum.tile([P, 512], F32, tag="ps")
-                    n = 0
-                    for a in range(2):
-                        for b in range(2):
-                            plus = (a == 1) if g == 2 else (a == b)
-                            nc.tensor.matmul(
-                                out=pd[:].rearrange("p (c j) -> p c j", j=8),
-                                lhsT=(half_p if plus else half_n)[:],
-                                rhs=xv[:, a, b],
-                                start=(n == 0),
-                                stop=(n == 3),
-                            )
-                            n += 1
-                    nc.scalar.copy(
-                        out=gd[:, tt, g].rearrange("p (m q) t -> p m q t", m=2),
-                        in_=pd[:].rearrange("p (m t q) -> p m q t", m=2, t=4),
+                        out=raw[:, g : g + step, :].bitcast(I32),
+                        in_=w1_dram[:, g : g + step, 2048 * gg : 2048 * (gg + 1)].bitcast(I32),
                     )
 
-            sums = {}
+            for gg in range(4):
+                load_w1(gg)
 
-            def dwt_rows(m):
-                if m % 2 == 0:
-                    s_t = head.tile([P, 2, 8, 16, 4], F32, tag="s", bufs=2)
-                    sums[m // 2] = s_t
-                nc.vector.tensor_scalar_mul(
-                    out=xh[:, m].rearrange("p t q -> p (t q)"), in0=x_sb[:, m].rearrange("p t q -> p (t q)"), scalar1=0.5
+            nc.vector.tensor_scalar_mul(out=half_i[:], in0=ident[:], scalar1=0.5)
+            hv = half_i[:].rearrange("p (i a r) -> p a i r", i=4, a=2)
+            for s, op in ((0, ALU.add), (1, ALU.subtract)):
+                nc.vector.tensor_tensor(
+                    out=rows_sd[:, s, :].rearrange("p (i r) -> p i r", i=4), in0=hv[:, 1], in1=hv[:, 0], op=op
                 )
-                xv = xh[:, m].rearrange("p t (i a r) -> p i a r t", a=2, r=16)
-                nc.vector.tensor_tensor(out=sums[m // 2][:, m % 2], in0=xv[:, :, 0], in1=xv[:, :, 1], op=ALU.add)
+            rv = rows_sd[:].rearrange("p s (q b) -> p s q b", b=2)
+            for s, op in ((0, ALU.add), (1, ALU.subtract)):
+                nc.vector.tensor_tensor(
+                    out=haar[:].rearrange("p (d s) q -> p d s q", s=2)[:, :, s, :],
+                    in0=rv[:, :, :, 1],
+                    in1=rv[:, :, :, 0],
+                    op=op,
+                )
 
-            def dwt_cols(tt):
-                sv = sums[tt][:].rearrange("p m i (j b) t -> p (m i j) b t", b=2)
-                nc.vector.tensor_tensor(out=gd[:, tt, 0], in0=sv[:, :, 1], in1=sv[:, :, 0], op=ALU.add)
-                nc.vector.tensor_tensor(out=gd[:, tt, 1], in0=sv[:, :, 1], in1=sv[:, :, 0], op=ALU.subtract)
+            ptx = {}
+            pdx = {}
 
-            def quant_d(tt):
+            def copy_on(engine, out_ap, in_ap):
+                if engine == "v":
+                    nc.vector.tensor_copy(out=out_ap, in_=in_ap)
+                else:
+                    nc.scalar.copy(out=out_ap, in_=in_ap)
+
+            def tr_x(mh):
+                pt = psum.tile([P, 4, 128], BF16, tag="ps")
+                for t in range(4):
+                    nc.tensor.transpose(
+                        out=pt[:, t, :],
+                        in_=x_sb[:, mh // 2, t, 128 * (mh % 2) : 128 * (mh % 2) + 128],
+                        identity=ident[:],
+                    )
+                ptx[mh] = pt
+
+            def ev_x(mh, engine):
+                copy_on(engine, x_t[:, mh], ptx[mh][:])
+
+            def mm_h(mh):
+                pd = psum.tile([P, 4, 128], F32, tag="ps")
+                for t in range(4):
+                    nc.tensor.matmul(
+                        out=pd[:, t, :],
+                        lhsT=x_t[:, mh, t, :],
+                        rhs=haar[:].rearrange("p g q -> p (g q)"),
+                        start=True,
+                        stop=True,
+                    )
+                pdx[mh] = pd
+
+            def ev_d(mh, engine):
+                copy_on(
+                    engine,
+                    gd[:, :, 32 * mh : 32 * mh + 32, :],
+                    pdx[mh][:].rearrange("p t (g q) -> p g q t", g=4),
+                )
+
+            def q_d(tt):
+                for g in range(4):
+                    nc.vector.quantize_mx(
+                        out=dq[:, g, 128 * tt : 128 * tt + 128].bitcast(FP8X4),
+                        scales=dsc[:, g, 128 * tt : 128 * tt + 128],
+                        in_=gd[:, g, 128 * tt : 128 * tt + 128, :].rearrange("p w t -> p (w t)"),
+                    )
+
+            def perm_w(gg, g0=0, g1=4):
+                nc.vector.tensor_copy(
+                    out=w1p[:, gg, g0:g1, :].rearrange("p g (t m) -> p g m t", t=4).bitcast(I32),
+                    in_=raws[gg][:, g0:g1, :].rearrange("p g (m t) -> p g m t", t=4).bitcast(I32),
+                )
+
+            def perm_s(c0, c1):
+                nc.vector.tensor_copy(
+                    out=w1sp[:, c0:c1].rearrange("p (k t m) -> p k m t", t=4, m=128),
+                    in_=w1s[:, c0:c1].rearrange("p (k m t) -> p k m t", t=4, m=128),
+                )
+
+            def mm1(gg, lo, hi):
+                for t in range(4):
+                    if lo == 0:
+                        acc = psum.tile([P, 256], F32, tag="ps")
+                        accs[(gg, t)] = acc
+                    for g in range(4):
+                        nc.tensor.matmul_mx(
+                            out=accs[(gg, t)][:, lo:hi],
+                            lhsT=w1p[:, gg, g, 128 * t : 128 * t + 128].bitcast(FP8X4),
+                            lhsT_scale=w1sp[4 * g : P, 512 * gg + 128 * t : 512 * gg + 128 * t + 128],
+                            rhs=dq[:, g, lo:hi].bitcast(FP8X4),
+                            rhs_scale=dsc[:, g, lo:hi],
+                            start=(g == 0),
+                            stop=(g == 3),
+                        )
+
+            def si(gg):
+                fpl = work.tile([P, 4, 256], BF16, tag="fpl", bufs=4)
+                for t in range(4):
+                    nc.scalar.activation(
+                        out=fpl[:, t, :],
+                        in_=accs[(gg, t)][:],
+                        func=ACT.Silu,
+                        bias=b1t[:, 4 * gg + t : 4 * gg + t + 1],
+                    )
+                fpls[gg] = fpl
+
+            def rg(gg):
+                gf = work.tile([P, 256, 4], BF16, tag="gf", bufs=4, align_bytes=64)
+                for engine, lo, hi in (("s", 128, 256), ("v", 0, 128)):
+                    copy_on(
+                        engine,
+                        gf[:, lo:hi, :].rearrange("p (c i) t -> p c t i", i=4),
+                        fpls[gg][:, :, lo:hi].rearrange("p t (c i) -> p c t i", i=4),
+                    )
+                gfs[gg] = gf
+
+            def qf(gg):
                 nc.vector.quantize_mx(
-                    out=dq[:, tt].rearrange("p g w -> p (g w)").bitcast(FP8X4),
-                    scales=dsc[:, tt].rearrange("p g w -> p (g w)"),
-                    in_=gd[:, tt].rearrange("p g w t -> p (g w t)"),
+                    out=fq[:, gg, :].bitcast(FP8X4),
+                    scales=fsc[:, gg, :],
+                    in_=gfs[gg][:].rearrange("p w t -> p (w t)"),
                 )
 
             pw = psum.tile([P, 512], F32, tag="ps")
-            for n in range(8):
+            for n in range(4):
                 nc.tensor.matmul(out=pw[:], lhsT=wz[:, 0:P], rhs=wz[:], start=True, stop=True)
-            dwt_pe(0)
-            dwt_pe(1)
-            dwt_rows(0)
-            dwt_rows(1)
-            dwt_cols(0)
-            dwt_rows(2)
-            quant_d(0)
-            dwt_rows(3)
-            dwt_cols(1)
-            quant_d(1)
+            tr_x(0)
+            tr_x(1)
+            ev_x(0, "v")
+            ev_x(1, "s")
+            tr_x(2)
+            tr_x(3)
+            mm_h(0)
+            mm_h(1)
+            ev_x(2, "v")
+            ev_x(3, "s")
+            ev_d(0, "v")
+            ev_d(1, "s")
+            tr_x(4)
+            tr_x(5)
+            mm_h(2)
+            mm_h(3)
+            ev_d(2, "s")
+            ev_d(3, "s")
+            ev_x(4, "v")
+            ev_x(5, "s")
+            tr_x(6)
+            tr_x(7)
+            mm_h(4)
+            mm_h(5)
+            ev_x(6, "v")
+            ev_x(7, "s")
+            perm_w(0, 0, 1)
+            perm_w(0, 1, 2)
+            q_d(0)
+            perm_w(0, 2, 3)
+            perm_w(0, 3, 4)
+            perm_s(0, 1024)
+            mm_h(6)
+            mm_h(7)
+            ev_d(4, "s")
+            ev_d(5, "s")
+            ev_d(6, "v")
+            ev_d(7, "v")
+            q_d(1)
 
             ptb = psum.tile([P, 5, 128], BF16, tag="ps")
             for t in range(4):
-                nc.tensor.transpose(out=ptb[:, t, :], in_=bs[:, t, :], identity=ident_b[:])
-            nc.tensor.transpose(out=ptb[:, 4, :], in_=bz[:, 512:640], identity=ident_b[:])
+                nc.tensor.transpose(out=ptb[:, t, :], in_=bz[:, t:512:4], identity=ident[:])
+            nc.tensor.transpose(out=ptb[:, 4, :], in_=bz[:, 512:640], identity=ident[:])
             nc.scalar.copy(
                 out=b1t[:].rearrange("p (g t) -> p g t", t=4), in_=ptb[:, 0:4, 0:8].rearrange("p t g -> p g t")
             )
@@ -191,150 +289,44 @@ def tile_waveletblock_w_kernel(tc, x, w1_words, w1_scales, b1, w2_words, w2_scal
             nc.gpsimd.tensor_tensor(out=bias_p2[:], in0=bias_4p[:], in1=bias_4p[:], op=ALU.add)
             nc.gpsimd.tensor_tensor(out=bias_m2[:], in0=bias_4m[:], in1=bias_4m[:], op=ALU.add)
 
-        work = ctx.enter_context(tc.tile_pool(name="work", bufs=1))
+            mm1(0, 0, 128)
+            mm1(0, 128, 256)
+            perm_w(1)
+            load_w1(4)
+            for gg in range(1, 8):
+                mm1(gg, 0, 256)
+                si(gg - 1)
+                if gg % 2 == 1 and gg < 7:
+                    perm_s(512 * (gg + 1), 512 * (gg + 3))
+                if gg < 7:
+                    perm_w(gg + 1)
+                    if gg + 4 < 8:
+                        load_w1(gg + 4)
+                rg(gg - 1)
+                qf(gg - 1)
+
+        for s in (1, 2, 3):
+            for h in range(4):
+                nc.sync.dma_start(
+                    out=w2[:, 2 * h : 2 * h + 2, 512 * s : 512 * (s + 1)].bitcast(I32),
+                    in_=w2_dram[:, 2 * h : 2 * h + 2, 2048 * s : 2048 * (s + 1)].bitcast(I32),
+                )
+        for h in range(2):
+            nc.sync.dma_start(
+                out=w2[:, :, 256 * h : 256 * (h + 1)].bitcast(I32),
+                in_=w2_dram[:, :, 1024 * h : 1024 * (h + 1)].bitcast(I32),
+            )
+
         fin = ctx.enter_context(tc.tile_pool(name="fin", bufs=1))
 
-        accs = {}
-        pres = {}
-        tps = {}
-        fpls = {}
-        gfs = {}
-
-        def mm1_pass(nt, tt, g):
-            if g == 0:
-                acc = psum.tile([P, 512], F32, tag="ps")
-                accs[(nt, tt)] = acc
-            nc.tensor.matmul_mx(
-                out=accs[(nt, tt)][:],
-                lhsT=dq[:, tt, g, :].bitcast(FP8X4),
-                lhsT_scale=dsc[:, tt, g, :],
-                rhs=w1[:, g, 512 * nt : 512 * (nt + 1)].bitcast(FP8X4),
-                rhs_scale=w1s[4 * g : P, 512 * nt : 512 * (nt + 1)],
-                start=(g == 0),
-                stop=(g == 3),
-            )
-
-        def mm1(nt):
-            for tt in range(2):
-                for g in range(4):
-                    mm1_pass(nt, tt, g)
-
-        def cp(nt):
-            for tt in range(2):
-                pre = work.tile([P, 4, 128], F32, tag="pre", bufs=8)
-                src = accs[(nt, tt)][:].rearrange("q (p t) -> q t p", t=4)
-                if tt == 0:
-                    nc.vector.tensor_copy(out=pre[:], in_=src)
-                else:
-                    nc.scalar.copy(out=pre[:], in_=src)
-                pres[(nt, tt)] = pre
-
-        def tr(nt):
-            for tp2 in range(2):
-                tpf = psum.tile([P, 2, 256], F32, tag="ps")
-                for t2 in range(2):
-                    for tt in range(2):
-                        nc.tensor.transpose(
-                            out=tpf[:, t2, 128 * tt : 128 * (tt + 1)],
-                            in_=pres[(nt, tt)][:, 2 * tp2 + t2, :],
-                            identity=ident_f[:],
-                        )
-                tps[(nt, tp2)] = tpf
-
-        def si(nt):
-            fpl = work.tile([P, 4, 256], BF16, tag="fpl", bufs=4)
-            for t in range(4):
-                nc.scalar.activation(
-                    out=fpl[:, t, :],
-                    in_=tps[(nt, t // 2)][:, t % 2, :],
-                    func=ACT.Silu,
-                    bias=b1t[:, 4 * nt + t : 4 * nt + t + 1],
-                )
-            fpls[nt] = fpl
-
-        def rg(nt):
-            gf = work.tile([P, 256, 4], BF16, tag="gf", bufs=4, align_bytes=64)
-            nc.vector.tensor_copy(
-                out=gf[:].rearrange("p (c i) t -> p c t i", i=4),
-                in_=fpls[nt][:].rearrange("p t (c i) -> p c t i", i=4),
-            )
-            gfs[nt] = gf
-
-        def qf(nt):
-            nc.vector.quantize_mx(
-                out=fq[:, nt, :].bitcast(FP8X4),
-                scales=fsc[:, nt, :],
-                in_=gfs[nt][:].rearrange("p w t -> p (w t)"),
-            )
-
-        for g in range(3):
-            for nt in range(2):
-                mm1_pass(nt, 0, g)
-        for g in range(3):
-            for nt in range(2):
-                mm1_pass(nt, 1, g)
-        for tt in range(2):
-            for nt in range(2):
-                mm1_pass(nt, tt, 3)
-        cp(0)
-        cp(1)
-        for g in range(2):
-            for nt in (2, 3):
-                for tt in range(2):
-                    mm1_pass(nt, tt, g)
-        tr(0)
-        tr(1)
-        si(0)
-        si(1)
-        for g in (2, 3):
-            for nt in (2, 3):
-                for tt in range(2):
-                    mm1_pass(nt, tt, g)
-        cp(2)
-        cp(3)
-        rg(0)
-        rg(1)
-        qf(0)
-        qf(1)
-        for g in range(2):
-            for nt in (4, 5):
-                for tt in range(2):
-                    mm1_pass(nt, tt, g)
-        tr(2)
-        tr(3)
-        si(2)
-        si(3)
-        for g in (2, 3):
-            for nt in (4, 5):
-                for tt in range(2):
-                    mm1_pass(nt, tt, g)
-        cp(4)
-        cp(5)
-        rg(2)
-        rg(3)
-        qf(2)
-        qf(3)
-        mm1(6)
-        cp(6)
-        tr(4)
-        tr(5)
-        si(4)
-        si(5)
-        mm1(7)
-        cp(7)
-        rg(4)
-        rg(5)
-        qf(4)
-        qf(5)
-
-        def mm2(acc, s, ct, g):
+        def mm2(acc, s, ct, g, lo=0, hi=256):
             m0 = 512 * s + 128 * ct
             nc.tensor.matmul_mx(
-                out=acc[:],
+                out=acc,
                 lhsT=w2[:, g, m0 : m0 + 128].bitcast(FP8X4),
                 lhsT_scale=w2s[4 * (g % 4) : P, g // 4, m0 : m0 + 128],
-                rhs=fq[:, g, :].bitcast(FP8X4),
-                rhs_scale=fsc[:, g, :],
+                rhs=fq[:, g, lo:hi].bitcast(FP8X4),
+                rhs_scale=fsc[:, g, lo:hi],
                 start=(g == 0),
                 stop=(g == 7),
             )
@@ -346,31 +338,14 @@ def tile_waveletblock_w_kernel(tc, x, w1_words, w1_scales, b1, w2_words, w2_scal
         for ct in range(4):
             acc_a = psum.tile([P, 256], F32, tag="ps")
             first.append(acc_a)
-        for g in range(2):
+        for g in range(7):
             for ct in range(4):
-                mm2(first[ct], 1, ct, g)
-        tr(6)
-        tr(7)
-        si(6)
+                mm2(first[ct][:], 1, ct, g)
         si(7)
-        rg(6)
-        qf(6)
         rg(7)
         qf(7)
-        for g in range(2, 6):
-            for ct in range(4):
-                mm2(first[ct], 1, ct, g)
-        second = []
-        for ct in range(2):
-            acc_b = psum.tile([P, 256], F32, tag="ps")
-            second.append(acc_b)
-            for g in range(6):
-                mm2(acc_b, 2, ct, g)
-        for g in range(6, 8):
-            for ct in range(4):
-                mm2(first[ct], 1, ct, g)
-            for ct in range(2):
-                mm2(second[ct], 2, ct, g)
+        for ct in range(4):
+            mm2(first[ct][:], 1, ct, 7)
         for ct in range(4):
             nc.scalar.activation(
                 out=y2s[:, ct, :], in_=first[ct][:], func=ACT.Identity, bias=bias_e[:, ct : ct + 1], scale=0.5
@@ -380,12 +355,9 @@ def tile_waveletblock_w_kernel(tc, x, w1_words, w1_scales, b1, w2_words, w2_scal
             )
 
         for ct in range(4):
-            if ct < 2:
-                acc_b = second[ct]
-            else:
-                acc_b = psum.tile([P, 256], F32, tag="ps")
-                for g in range(8):
-                    mm2(acc_b, 2, ct, g)
+            acc_b = psum.tile([P, 256], F32, tag="ps")
+            for g in range(8):
+                mm2(acc_b[:], 2, ct, g)
             nc.vector.scalar_tensor_tensor(
                 out=y2s[:, ct, :], in0=acc_b[:], scalar=0.5, in1=y2s[:, ct, :], op0=ALU.mult, op1=ALU.add
             )
@@ -398,7 +370,7 @@ def tile_waveletblock_w_kernel(tc, x, w1_words, w1_scales, b1, w2_words, w2_scal
         def third(ct):
             acc_c = psum.tile([P, 256], F32, tag="ps")
             for g in range(8):
-                mm2(acc_c, 3, ct, g)
+                mm2(acc_c[:], 3, ct, g)
             y4p = fin.tile([P, 256], F32, tag="y4p", bufs=2)
             y4m = fin.tile([P, 256], F32, tag="y4m", bufs=2)
             nc.scalar.activation(out=y4p[:], in_=acc_c[:], func=ACT.Identity, bias=bias_p2[:, ct : ct + 1], scale=0.5)
@@ -414,24 +386,33 @@ def tile_waveletblock_w_kernel(tc, x, w1_words, w1_scales, b1, w2_words, w2_scal
             nc.gpsimd.tensor_tensor(out=t_t[:, 3, :], in0=y4p[:], in1=y2s[:, ct, :], op=ALU.add)
             planes[ct] = t_t
 
-        def last(ct):
-            acc_d = psum.tile([P, 256], F32, tag="ps")
-            for g in range(8):
-                mm2(acc_d, 0, ct, g)
+        def last(ct, pieces):
             o_t = fin.tile([P, 4, 8, 2, 8, 2], F32, tag="o", bufs=3)
-            for a in range(2):
-                nc.vector.scalar_tensor_tensor(
-                    out=o_t[:, :, :, a].rearrange("p m i j b -> p (m i) j b"),
-                    in0=acc_d[:].rearrange("p (q j) -> p q j", j=8).unsqueeze(3).to_broadcast([P, 32, 8, 2]),
-                    scalar=0.5,
-                    in1=planes[ct][:, 2 * a : 2 * a + 2, :].rearrange("p b (q j) -> p q j b", j=8),
-                    op0=ALU.mult,
-                    op1=ALU.add,
+            images = 4 // pieces
+            for h in range(pieces):
+                lo, hi = 64 * images * h, 64 * images * (h + 1)
+                m0, m1 = images * h, images * (h + 1)
+                acc_d = psum.tile([P, 64 * images], F32, tag="ps")
+                for g in range(8):
+                    mm2(acc_d[:], 0, ct, g, lo, hi)
+                for a in range(2):
+                    nc.vector.scalar_tensor_tensor(
+                        out=o_t[:, m0:m1, :, a].rearrange("p m i j b -> p (m i) j b"),
+                        in0=acc_d[:]
+                        .rearrange("p (q j) -> p q j", j=8)
+                        .unsqueeze(3)
+                        .to_broadcast([P, 8 * images, 8, 2]),
+                        scalar=0.5,
+                        in1=planes[ct][:, 2 * a : 2 * a + 2, lo:hi].rearrange("p b (q j) -> p q j b", j=8),
+                        op0=ALU.mult,
+                        op1=ALU.add,
+                    )
+                nc.sync.dma_start(
+                    out=out_dram[ct][:, m0:m1, :], in_=o_t[:, m0:m1].rearrange("p m i a j b -> p m (i a j b)")
                 )
-            nc.sync.dma_start(out=out_dram[ct], in_=o_t[:].rearrange("p m i a j b -> p m (i a j b)"))
 
         for pair in range(2):
             third(2 * pair)
             third(2 * pair + 1)
-            last(2 * pair)
-            last(2 * pair + 1)
+            last(2 * pair, 1)
+            last(2 * pair + 1, 1 + pair)

@@ -24,10 +24,10 @@ def tile_waveletblock_w_kernel(tc, x, w1_words, w1_scales, b1, w2_words, w2_scal
         work = ctx.enter_context(tc.tile_pool(name="work", bufs=1))
         psum = ctx.enter_context(tc.psum_pool(name="psum", bufs=8))
 
-        w1p = keep.tile([P, 8, 4, 512], U32, align_bytes=64)
+        w1p = keep.tile([P, 8, 4, 4, 128], U32, align_bytes=64)
         w2 = keep.tile([P, 8, 2048], U32, align_bytes=64)
         w1s = keep.tile([P, 4096], U8, align_bytes=64)
-        w1sp = keep.tile([P, 4096], U8, align_bytes=64)
+        w1sp = keep.tile([P, 4, 4, 2, 128], U8, align_bytes=64)
         w2s = keep.tile([P, 2, 2048], U8, align_bytes=64)
         dq = keep.tile([P, 4, 256], U32, align_bytes=64)
         dsc = keep.tile([P, 4, 256], U8, align_bytes=64)
@@ -48,7 +48,7 @@ def tile_waveletblock_w_kernel(tc, x, w1_words, w1_scales, b1, w2_words, w2_scal
         bias_f = keep.tile([P, 4], F32)
         bias_p2 = keep.tile([P, 4], F32)
         bias_m2 = keep.tile([P, 4], F32)
-        wz = keep.tile([P, 512], BF16)
+        wz = keep.tile([P, 128], BF16)
         warm_in = keep.tile([P, 1], F32)
         warm_out = keep.tile([P, 1], F32)
 
@@ -64,7 +64,9 @@ def tile_waveletblock_w_kernel(tc, x, w1_words, w1_scales, b1, w2_words, w2_scal
         with tc.tile_pool(name="head", bufs=1) as head:
             x_sb = head.tile([P, 4, 4, 256], BF16)
             x_t = head.tile([P, 8, 4, 128], BF16)
-            gd = head.tile([P, 4, 256, 4], BF16, align_bytes=64)
+            gd0 = head.tile([P, 4, 128, 4], BF16, align_bytes=64)
+            gd1 = head.tile([P, 4, 128, 4], BF16, align_bytes=64)
+            gd = (gd0, gd1)
 
             nc.vector.memset(warm_in[:], 0.0)
             nc.vector.memset(wz[:], 0.0)
@@ -82,7 +84,7 @@ def tile_waveletblock_w_kernel(tc, x, w1_words, w1_scales, b1, w2_words, w2_scal
                     out=w1s[32 * q : 32 * q + 16, 1024:4096].bitcast(F32),
                     in_=w1_scales[:, 4 * q : 4 * q + 4, 1024:4096].bitcast(F32),
                 )
-            nc.vector.memset(w2s[:].bitcast(I32), 0)
+            nc.gpsimd.memset(w2s[:].bitcast(I32), 0)
             for h in range(2):
                 for q in range(4):
                     nc.gpsimd.dma_start(
@@ -161,7 +163,7 @@ def tile_waveletblock_w_kernel(tc, x, w1_words, w1_scales, b1, w2_words, w2_scal
             def ev_d(mh, engine):
                 copy_on(
                     engine,
-                    gd[:, :, 32 * mh : 32 * mh + 32, :],
+                    gd[mh // 4][:, :, 32 * (mh % 4) : 32 * (mh % 4) + 32, :],
                     pdx[mh][:].rearrange("p t (g q) -> p g q t", g=4),
                 )
 
@@ -170,19 +172,19 @@ def tile_waveletblock_w_kernel(tc, x, w1_words, w1_scales, b1, w2_words, w2_scal
                     nc.vector.quantize_mx(
                         out=dq[:, g, 128 * tt : 128 * tt + 128].bitcast(FP8X4),
                         scales=dsc[:, g, 128 * tt : 128 * tt + 128],
-                        in_=gd[:, g, 128 * tt : 128 * tt + 128, :].rearrange("p w t -> p (w t)"),
+                        in_=gd[tt][:, g].rearrange("p w t -> p (w t)"),
                     )
 
             def perm_w(gg, g0=0, g1=4):
                 nc.vector.tensor_copy(
-                    out=w1p[:, gg, g0:g1, :].rearrange("p g (t m) -> p g m t", t=4).bitcast(I32),
-                    in_=raws[gg][:, g0:g1, :].rearrange("p g (m t) -> p g m t", t=4).bitcast(I32),
+                    out=w1p[:, gg, :, g0:g1, :].bitcast(I32).rearrange("p t g (c i) -> p (g c) t i", i=4),
+                    in_=raws[gg][:, g0:g1, :].bitcast(I32).rearrange("p g (c i t) -> p (g c) t i", t=4, i=4),
                 )
 
-            def perm_s(c0, c1):
+            def perm_s(pair):
                 nc.vector.tensor_copy(
-                    out=w1sp[:, c0:c1].rearrange("p (k t m) -> p k m t", t=4, m=128),
-                    in_=w1s[:, c0:c1].rearrange("p (k m t) -> p k m t", t=4, m=128),
+                    out=w1sp[:, pair].rearrange("p t k (c i) -> p (k c) t i", i=16),
+                    in_=w1s[:, 1024 * pair : 1024 * (pair + 1)].rearrange("p (c i t) -> p c t i", t=4, i=16),
                 )
 
             def mm1(gg, lo, hi):
@@ -193,8 +195,8 @@ def tile_waveletblock_w_kernel(tc, x, w1_words, w1_scales, b1, w2_words, w2_scal
                     for g in range(4):
                         nc.tensor.matmul_mx(
                             out=accs[(gg, t)][:, lo:hi],
-                            lhsT=w1p[:, gg, g, 128 * t : 128 * t + 128].bitcast(FP8X4),
-                            lhsT_scale=w1sp[4 * g : P, 512 * gg + 128 * t : 512 * gg + 128 * t + 128],
+                            lhsT=w1p[:, gg, t, g, :].bitcast(FP8X4),
+                            lhsT_scale=w1sp[4 * g : P, gg // 2, t, gg % 2, :],
                             rhs=dq[:, g, lo:hi].bitcast(FP8X4),
                             rhs_scale=dsc[:, g, lo:hi],
                             start=(g == 0),
@@ -230,46 +232,29 @@ def tile_waveletblock_w_kernel(tc, x, w1_words, w1_scales, b1, w2_words, w2_scal
                 )
 
             pw = psum.tile([P, 512], F32, tag="ps")
-            for n in range(4):
-                nc.tensor.matmul(out=pw[:], lhsT=wz[:, 0:P], rhs=wz[:], start=True, stop=True)
-            tr_x(0)
-            tr_x(1)
-            ev_x(0, "v")
-            ev_x(1, "s")
-            tr_x(2)
-            tr_x(3)
-            mm_h(0)
-            mm_h(1)
-            ev_x(2, "v")
-            ev_x(3, "s")
-            ev_d(0, "v")
-            ev_d(1, "s")
-            tr_x(4)
-            tr_x(5)
-            mm_h(2)
-            mm_h(3)
-            ev_d(2, "s")
-            ev_d(3, "s")
-            ev_x(4, "v")
-            ev_x(5, "s")
-            tr_x(6)
-            tr_x(7)
-            mm_h(4)
-            mm_h(5)
-            ev_x(6, "v")
-            ev_x(7, "s")
-            perm_w(0, 0, 1)
-            perm_w(0, 1, 2)
+            for n in range(3):
+                nc.tensor.matmul(
+                    out=pw[:].rearrange("p (r c) -> p r c", r=4),
+                    lhsT=wz[:],
+                    rhs=wz[:].unsqueeze(1).to_broadcast([P, 4, 128]),
+                    start=True,
+                    stop=True,
+                )
+            for m in range(5):
+                if m < 4:
+                    tr_x(2 * m)
+                    tr_x(2 * m + 1)
+                    ev_x(2 * m, "v")
+                    ev_x(2 * m + 1, "v")
+                if m > 0:
+                    mm_h(2 * m - 2)
+                    mm_h(2 * m - 1)
+                    ev_d(2 * m - 2, "s")
+                    ev_d(2 * m - 1, "s")
+            perm_w(0, 0, 2)
             q_d(0)
-            perm_w(0, 2, 3)
-            perm_w(0, 3, 4)
-            perm_s(0, 1024)
-            mm_h(6)
-            mm_h(7)
-            ev_d(4, "s")
-            ev_d(5, "s")
-            ev_d(6, "v")
-            ev_d(7, "v")
+            perm_w(0, 2, 4)
+            perm_s(0)
             q_d(1)
 
             ptb = psum.tile([P, 5, 128], BF16, tag="ps")
@@ -296,9 +281,9 @@ def tile_waveletblock_w_kernel(tc, x, w1_words, w1_scales, b1, w2_words, w2_scal
             for gg in range(1, 8):
                 mm1(gg, 0, 256)
                 si(gg - 1)
-                if gg % 2 == 1 and gg < 7:
-                    perm_s(512 * (gg + 1), 512 * (gg + 3))
                 if gg < 7:
+                    if gg % 2 == 1:
+                        perm_s((gg + 1) // 2)
                     perm_w(gg + 1)
                     if gg + 4 < 8:
                         load_w1(gg + 4)
@@ -414,5 +399,5 @@ def tile_waveletblock_w_kernel(tc, x, w1_words, w1_scales, b1, w2_words, w2_scal
         for pair in range(2):
             third(2 * pair)
             third(2 * pair + 1)
-            last(2 * pair, 1)
+            last(2 * pair, 1 + pair)
             last(2 * pair + 1, 1 + pair)

@@ -216,7 +216,7 @@ def tile_waveletblock_w_kernel(tc, x, w1_words, w1_scales, b1, w2_words, w2_scal
 
             def rg(gg):
                 gf = work.tile([P, 256, 4], BF16, tag="gf", bufs=4, align_bytes=64)
-                for engine, lo, hi in (("s", 128, 256), ("v", 0, 128)):
+                for engine, lo, hi in (("s", 0, 256),) if gg < 7 else (("s", 128, 256), ("v", 0, 128)):
                     copy_on(
                         engine,
                         gf[:, lo:hi, :].rearrange("p (c i) t -> p c t i", i=4),
@@ -290,12 +290,16 @@ def tile_waveletblock_w_kernel(tc, x, w1_words, w1_scales, b1, w2_words, w2_scal
                 rg(gg - 1)
                 qf(gg - 1)
 
-        for s in (1, 2, 3):
-            for h in range(4):
-                nc.sync.dma_start(
-                    out=w2[:, 2 * h : 2 * h + 2, 512 * s : 512 * (s + 1)].bitcast(I32),
-                    in_=w2_dram[:, 2 * h : 2 * h + 2, 2048 * s : 2048 * (s + 1)].bitcast(I32),
-                )
+        for h in range(4):
+            nc.sync.dma_start(
+                out=w2[:, 2 * h : 2 * h + 2, 512:1536].bitcast(I32),
+                in_=w2_dram[:, 2 * h : 2 * h + 2, 2048:6144].bitcast(I32),
+            )
+        for h in range(2):
+            nc.sync.dma_start(
+                out=w2[:, 4 * h : 4 * h + 4, 1536:2048].bitcast(I32),
+                in_=w2_dram[:, 4 * h : 4 * h + 4, 6144:8192].bitcast(I32),
+            )
         for h in range(2):
             nc.sync.dma_start(
                 out=w2[:, :, 256 * h : 256 * (h + 1)].bitcast(I32),
@@ -323,14 +327,26 @@ def tile_waveletblock_w_kernel(tc, x, w1_words, w1_scales, b1, w2_words, w2_scal
         for ct in range(4):
             acc_a = psum.tile([P, 256], F32, tag="ps")
             first.append(acc_a)
-        for g in range(7):
+        for g in range(4):
             for ct in range(4):
                 mm2(first[ct][:], 1, ct, g)
         si(7)
         rg(7)
         qf(7)
+        second = []
         for ct in range(4):
-            mm2(first[ct][:], 1, ct, 7)
+            acc_b = psum.tile([P, 256], F32, tag="ps")
+            second.append(acc_b)
+        for g in range(4):
+            for ct in range(4):
+                mm2(second[ct][:], 2, ct, g)
+        for g in range(4, 8):
+            for ct in range(4):
+                mm2(first[ct][:], 1, ct, g)
+            if g % 2 == 1:
+                for h in (g - 1, g):
+                    for ct in range(4):
+                        mm2(second[ct][:], 2, ct, h)
         for ct in range(4):
             nc.scalar.activation(
                 out=y2s[:, ct, :], in_=first[ct][:], func=ACT.Identity, bias=bias_e[:, ct : ct + 1], scale=0.5
@@ -340,9 +356,7 @@ def tile_waveletblock_w_kernel(tc, x, w1_words, w1_scales, b1, w2_words, w2_scal
             )
 
         for ct in range(4):
-            acc_b = psum.tile([P, 256], F32, tag="ps")
-            for g in range(8):
-                mm2(acc_b[:], 2, ct, g)
+            acc_b = second[ct]
             nc.vector.scalar_tensor_tensor(
                 out=y2s[:, ct, :], in0=acc_b[:], scalar=0.5, in1=y2s[:, ct, :], op0=ALU.mult, op1=ALU.add
             )

from contextlib import ExitStack

import concourse.mybir as mybir
from concourse.masks import make_identity

F32 = mybir.dt.float32
BF16 = mybir.dt.bfloat16
I32 = mybir.dt.int32
U32 = mybir.dt.uint32
U8 = mybir.dt.uint8
FP8X4 = mybir.dt.float8_e4m3fn_x4
ALU = mybir.AluOpType
ACT = mybir.ActivationFunctionType

P = 128
FLOPS = 2 * 256 * 2048 * 4096 * 2


def tile_waveletblock_w_kernel(tc, x, w1_words, w1_scales, b1, w2_words, w2_scales, b2, out):
    nc = tc.nc
    with ExitStack() as ctx:
        ctx.enter_context(tc.manual_schedule())
        keep = ctx.enter_context(tc.tile_pool(name="keep", bufs=1))
        work = ctx.enter_context(tc.tile_pool(name="work", bufs=1))
        psum = ctx.enter_context(tc.psum_pool(name="psum", bufs=8))

        w1p = keep.tile([P, 8, 4, 4, 128], U32, align_bytes=64)
        w2 = keep.tile([P, 8, 2048], U32, align_bytes=64)
        w1s = keep.tile([P, 4096], U8, align_bytes=64)
        w1sp = keep.tile([P, 4, 4, 2, 128], U8, align_bytes=64)
        w2s = keep.tile([P, 2, 2048], U8, align_bytes=64)
        dq = keep.tile([P, 4, 256], U32, align_bytes=64)
        dsc = keep.tile([P, 4, 256], U8, align_bytes=64)
        fq = keep.tile([P, 8, 256], U32, align_bytes=64)
        fsc = keep.tile([P, 8, 256], U8, align_bytes=64)
        ident = keep.tile([P, P], BF16)
        half_i = keep.tile([P, P], BF16)
        rows_sd = keep.tile([P, 2, 64], BF16)
        haar = keep.tile([P, 4, 32], BF16)
        bz = keep.tile([P, 640], BF16)
        b1t = keep.tile([P, 32], F32)
        b2h = keep.tile([P, 16], F32)
        bias_2s = keep.tile([P, 4], F32)
        bias_2n = keep.tile([P, 4], F32)
        bias_4p = keep.tile([P, 4], F32)
        bias_4m = keep.tile([P, 4], F32)
        bias_e = keep.tile([P, 4], F32)
        bias_f = keep.tile([P, 4], F32)
        bias_p2 = keep.tile([P, 4], F32)
        bias_m2 = keep.tile([P, 4], F32)
        wz = keep.tile([P, 128], BF16)
        warm_in = keep.tile([P, 1], F32)
        warm_out = keep.tile([P, 1], F32)

        w1_dram = w1_words.rearrange("g p n t -> p g (n t)")
        w2_dram = w2_words.rearrange("g p n t -> p g (n t)")
        x_dram = x.rearrange("b l (p t) h w -> p (b l) (t h w)", t=4)
        out_dram = out.rearrange("b l (k c) h w -> k c (b l) (h w)", c=P)

        accs = {}
        fpls = {}
        gfs = {}

        with tc.tile_pool(name="head", bufs=1) as head:
            x_sb = head.tile([P, 4, 4, 256], BF16)
            x_t = head.tile([P, 8, 4, 128], BF16)
            gd0 = head.tile([P, 4, 128, 4], BF16, align_bytes=64)
            gd1 = head.tile([P, 4, 128, 4], BF16, align_bytes=64)
            gd = (gd0, gd1)

            nc.vector.memset(warm_in[:], 0.0)
            nc.vector.memset(wz[:], 0.0)
            nc.vector.memset(w1s[:].bitcast(I32), 0)
            nc.vector.memset(bz[:], 0.0)
            make_identity(nc, ident[:])

            for m in range(4):
                nc.sync.dma_start(out=x_sb[:, m].rearrange("p t q -> p (t q)"), in_=x_dram[:, m, :])
            nc.scalar.activation(out=warm_out[:], in_=warm_in[:], func=ACT.Silu)
            nc.scalar.dma_start(out=bz[0:8, 0:512], in_=b1.rearrange("(r c) -> r c", c=512))
            nc.scalar.dma_start(out=bz[0:16, 512:640], in_=b2.rearrange("(r c) -> r c", c=128))
            for q in range(4):
                nc.gpsimd.dma_start(
                    out=w1s[32 * q : 32 * q + 16, 1024:4096].bitcast(F32),
                    in_=w1_scales[:, 4 * q : 4 * q + 4, 1024:4096].bitcast(F32),
                )
            nc.gpsimd.memset(w2s[:].bitcast(I32), 0)
            for h in range(2):
                for q in range(4):
                    nc.gpsimd.dma_start(
                        out=w2s[32 * q : 32 * q + 16, h, :].bitcast(F32),
                        in_=w2_scales[4 * h : 4 * h + 4, 4 * q : 4 * q + 4, :].bitcast(F32),
                    )
            for q in range(4):
                nc.sync.dma_start(
                    out=w1s[32 * q : 32 * q + 16, 0:1024].bitcast(I32),
                    in_=w1_scales[:, 4 * q : 4 * q + 4, 0:1024].bitcast(I32),
                )
            raws = {}

            def load_w1(gg):
                raw = head.tile([P, 4, 512], U32, tag="raw", bufs=4, align_bytes=64)
                raws[gg] = raw
                step = 1 if gg == 0 else 4
                for g in range(0, 4, step):
                    nc.sync.dma_start(
                        out=raw[:, g : g + step, :].bitcast(I32),
                        in_=w1_dram[:, g : g + step, 2048 * gg : 2048 * (gg + 1)].bitcast(I32),
                    )

            for gg in range(4):
                load_w1(gg)

            nc.vector.tensor_scalar_mul(out=half_i[:], in0=ident[:], scalar1=0.5)
            hv = half_i[:].rearrange("p (i a r) -> p a i r", i=4, a=2)
            for s, op in ((0, ALU.add), (1, ALU.subtract)):
                nc.vector.tensor_tensor(
                    out=rows_sd[:, s, :].rearrange("p (i r) -> p i r", i=4), in0=hv[:, 1], in1=hv[:, 0], op=op
                )
            rv = rows_sd[:].rearrange("p s (q b) -> p s q b", b=2)
            for s, op in ((0, ALU.add), (1, ALU.subtract)):
                nc.vector.tensor_tensor(
                    out=haar[:].rearrange("p (d s) q -> p d s q", s=2)[:, :, s, :],
                    in0=rv[:, :, :, 1],
                    in1=rv[:, :, :, 0],
                    op=op,
                )

            ptx = {}
            pdx = {}

            def copy_on(engine, out_ap, in_ap):
                if engine == "v":
                    nc.vector.tensor_copy(out=out_ap, in_=in_ap)
                else:
                    nc.scalar.copy(out=out_ap, in_=in_ap)

            def tr_x(mh):
                pt = psum.tile([P, 4, 128], BF16, tag="ps")
                for t in range(4):
                    nc.tensor.transpose(
                        out=pt[:, t, :],
                        in_=x_sb[:, mh // 2, t, 128 * (mh % 2) : 128 * (mh % 2) + 128],
                        identity=ident[:],
                    )
                ptx[mh] = pt

            def ev_x(mh, engine):
                copy_on(engine, x_t[:, mh], ptx[mh][:])

            def mm_h(mh):
                pd = psum.tile([P, 4, 128], F32, tag="ps")
                for t in range(4):
                    nc.tensor.matmul(
                        out=pd[:, t, :],
                        lhsT=x_t[:, mh, t, :],
                        rhs=haar[:].rearrange("p g q -> p (g q)"),
                        start=True,
                        stop=True,
                    )
                pdx[mh] = pd

            def ev_d(mh, engine):
                copy_on(
                    engine,
                    gd[mh // 4][:, :, 32 * (mh % 4) : 32 * (mh % 4) + 32, :],
                    pdx[mh][:].rearrange("p t (g q) -> p g q t", g=4),
                )

            def q_d(tt):
                for g in range(4):
                    nc.vector.quantize_mx(
                        out=dq[:, g, 128 * tt : 128 * tt + 128].bitcast(FP8X4),
                        scales=dsc[:, g, 128 * tt : 128 * tt + 128],
                        in_=gd[tt][:, g].rearrange("p w t -> p (w t)"),
                    )

            def perm_w(gg, g0=0, g1=4):
                nc.vector.tensor_copy(
                    out=w1p[:, gg, :, g0:g1, :].bitcast(I32).rearrange("p t g (c i) -> p (g c) t i", i=4),
                    in_=raws[gg][:, g0:g1, :].bitcast(I32).rearrange("p g (c i t) -> p (g c) t i", t=4, i=4),
                )

            def perm_s(pair):
                nc.vector.tensor_copy(
                    out=w1sp[:, pair].rearrange("p t k (c i) -> p (k c) t i", i=16),
                    in_=w1s[:, 1024 * pair : 1024 * (pair + 1)].rearrange("p (c i t) -> p c t i", t=4, i=16),
                )

            def mm1(gg, lo, hi):
                for t in range(4):
                    if lo == 0:
                        acc = psum.tile([P, 256], F32, tag="ps")
                        accs[(gg, t)] = acc
                    for g in range(4):
                        nc.tensor.matmul_mx(
                            out=accs[(gg, t)][:, lo:hi],
                            lhsT=w1p[:, gg, t, g, :].bitcast(FP8X4),
                            lhsT_scale=w1sp[4 * g : P, gg // 2, t, gg % 2, :],
                            rhs=dq[:, g, lo:hi].bitcast(FP8X4),
                            rhs_scale=dsc[:, g, lo:hi],
                            start=(g == 0),
                            stop=(g == 3),
                        )

            def si(gg):
                fpl = work.tile([P, 4, 256], BF16, tag="fpl", bufs=4)
                for t in range(4):
                    nc.scalar.activation(
                        out=fpl[:, t, :],
                        in_=accs[(gg, t)][:],
                        func=ACT.Silu,
                        bias=b1t[:, 4 * gg + t : 4 * gg + t + 1],
                    )
                fpls[gg] = fpl

            def rg(gg):
                gf = work.tile([P, 256, 4], BF16, tag="gf", bufs=4, align_bytes=64)
                for engine, lo, hi in (("s", 0, 256),) if gg < 7 else (("s", 128, 256), ("v", 0, 128)):
                    copy_on(
                        engine,
                        gf[:, lo:hi, :].rearrange("p (c i) t -> p c t i", i=4),
                        fpls[gg][:, :, lo:hi].rearrange("p t (c i) -> p c t i", i=4),
                    )
                gfs[gg] = gf

            def qf(gg):
                nc.vector.quantize_mx(
                    out=fq[:, gg, :].bitcast(FP8X4),
                    scales=fsc[:, gg, :],
                    in_=gfs[gg][:].rearrange("p w t -> p (w t)"),
                )

            pw = psum.tile([P, 512], F32, tag="ps")
            for n in range(3):
                nc.tensor.matmul(
                    out=pw[:].rearrange("p (r c) -> p r c", r=4),
                    lhsT=wz[:],
                    rhs=wz[:].unsqueeze(1).to_broadcast([P, 4, 128]),
                    start=True,
                    stop=True,
                )
            for m in range(5):
                if m < 4:
                    tr_x(2 * m)
                    tr_x(2 * m + 1)
                    ev_x(2 * m, "v")
                    ev_x(2 * m + 1, "v")
                if m > 0:
                    mm_h(2 * m - 2)
                    mm_h(2 * m - 1)
                    ev_d(2 * m - 2, "s")
                    ev_d(2 * m - 1, "s")
            perm_w(0, 0, 2)
            q_d(0)
            perm_w(0, 2, 4)
            perm_s(0)
            q_d(1)

            ptb = psum.tile([P, 5, 128], BF16, tag="ps")
            for t in range(4):
                nc.tensor.transpose(out=ptb[:, t, :], in_=bz[:, t:512:4], identity=ident[:])
            nc.tensor.transpose(out=ptb[:, 4, :], in_=bz[:, 512:640], identity=ident[:])
            nc.scalar.copy(
                out=b1t[:].rearrange("p (g t) -> p g t", t=4), in_=ptb[:, 0:4, 0:8].rearrange("p t g -> p g t")
            )
            nc.scalar.activation(out=b2h[:], in_=ptb[:, 4, 0:16], func=ACT.Copy, scale=0.5)
            nc.gpsimd.tensor_tensor(out=bias_2s[:], in0=b2h[:, 8:12], in1=b2h[:, 4:8], op=ALU.add)
            nc.gpsimd.tensor_tensor(out=bias_2n[:], in0=b2h[:, 8:12], in1=b2h[:, 4:8], op=ALU.subtract)
            nc.gpsimd.tensor_tensor(out=bias_4p[:], in0=b2h[:, 0:4], in1=b2h[:, 12:16], op=ALU.add)
            nc.gpsimd.tensor_tensor(out=bias_4m[:], in0=b2h[:, 0:4], in1=b2h[:, 12:16], op=ALU.subtract)
            nc.gpsimd.tensor_tensor(out=bias_e[:], in0=bias_2s[:], in1=bias_4p[:], op=ALU.subtract)
            nc.gpsimd.tensor_tensor(out=bias_f[:], in0=bias_2n[:], in1=bias_4m[:], op=ALU.subtract)
            nc.gpsimd.tensor_tensor(out=bias_p2[:], in0=bias_4p[:], in1=bias_4p[:], op=ALU.add)
            nc.gpsimd.tensor_tensor(out=bias_m2[:], in0=bias_4m[:], in1=bias_4m[:], op=ALU.add)

            mm1(0, 0, 128)
            mm1(0, 128, 256)
            perm_w(1)
            load_w1(4)
            for gg in range(1, 8):
                mm1(gg, 0, 256)
                si(gg - 1)
                if gg < 7:
                    if gg % 2 == 1:
                        perm_s((gg + 1) // 2)
                    perm_w(gg + 1)
                    if gg + 4 < 8:
                        load_w1(gg + 4)
                rg(gg - 1)
                qf(gg - 1)

        for h in range(4):
            nc.sync.dma_start(
                out=w2[:, 2 * h : 2 * h + 2, 512:1536].bitcast(I32),
                in_=w2_dram[:, 2 * h : 2 * h + 2, 2048:6144].bitcast(I32),
            )
        for h in range(2):
            nc.sync.dma_start(
                out=w2[:, 4 * h : 4 * h + 4, 1536:2048].bitcast(I32),
                in_=w2_dram[:, 4 * h : 4 * h + 4, 6144:8192].bitcast(I32),
            )
        for h in range(2):
            nc.sync.dma_start(
                out=w2[:, :, 256 * h : 256 * (h + 1)].bitcast(I32),
                in_=w2_dram[:, :, 1024 * h : 1024 * (h + 1)].bitcast(I32),
            )

        fin = ctx.enter_context(tc.tile_pool(name="fin", bufs=1))

        def mm2(acc, s, ct, g, lo=0, hi=256):
            m0 = 512 * s + 128 * ct
            nc.tensor.matmul_mx(
                out=acc,
                lhsT=w2[:, g, m0 : m0 + 128].bitcast(FP8X4),
                lhsT_scale=w2s[4 * (g % 4) : P, g // 4, m0 : m0 + 128],
                rhs=fq[:, g, lo:hi].bitcast(FP8X4),
                rhs_scale=fsc[:, g, lo:hi],
                start=(g == 0),
                stop=(g == 7),
            )

        y2s = fin.tile([P, 4, 256], F32)
        y2n = fin.tile([P, 4, 256], F32)

        first = []
        for ct in range(4):
            acc_a = psum.tile([P, 256], F32, tag="ps")
            first.append(acc_a)
        for g in range(4):
            for ct in range(4):
                mm2(first[ct][:], 1, ct, g)
        si(7)
        rg(7)
        qf(7)
        second = []
        for ct in range(4):
            acc_b = psum.tile([P, 256], F32, tag="ps")
            second.append(acc_b)
        for g in range(4):
            for ct in range(4):
                mm2(second[ct][:], 2, ct, g)
        for g in range(4, 8):
            for ct in range(4):
                mm2(first[ct][:], 1, ct, g)
            if g % 2 == 1:
                for h in (g - 1, g):
                    for ct in range(4):
                        mm2(second[ct][:], 2, ct, h)
        for ct in range(4):
            nc.scalar.activation(
                out=y2s[:, ct, :], in_=first[ct][:], func=ACT.Identity, bias=bias_e[:, ct : ct + 1], scale=0.5
            )
            nc.scalar.activation(
                out=y2n[:, ct, :], in_=first[ct][:], func=ACT.Identity, bias=bias_f[:, ct : ct + 1], scale=-0.5
            )

        for ct in range(4):
            acc_b = second[ct]
            nc.vector.scalar_tensor_tensor(
                out=y2s[:, ct, :], in0=acc_b[:], scalar=0.5, in1=y2s[:, ct, :], op0=ALU.mult, op1=ALU.add
            )
            nc.vector.scalar_tensor_tensor(
                out=y2n[:, ct, :], in0=acc_b[:], scalar=0.5, in1=y2n[:, ct, :], op0=ALU.mult, op1=ALU.add
            )

        planes = {}

        def third(ct):
            acc_c = psum.tile([P, 256], F32, tag="ps")
            for g in range(8):
                mm2(acc_c[:], 3, ct, g)
            y4p = fin.tile([P, 256], F32, tag="y4p", bufs=2)
            y4m = fin.tile([P, 256], F32, tag="y4m", bufs=2)
            nc.scalar.activation(out=y4p[:], in_=acc_c[:], func=ACT.Identity, bias=bias_p2[:, ct : ct + 1], scale=0.5)
            nc.scalar.activation(out=y4m[:], in_=acc_c[:], func=ACT.Identity, bias=bias_m2[:, ct : ct + 1], scale=-0.5)
            t_t = fin.tile([P, 4, 256], F32, tag="t", bufs=4)
            nc.vector.scalar_tensor_tensor(
                out=t_t[:, 0, :], in0=acc_c[:], scalar=0.5, in1=y2s[:, ct, :], op0=ALU.mult, op1=ALU.subtract
            )
            nc.vector.scalar_tensor_tensor(
                out=t_t[:, 1, :], in0=acc_c[:], scalar=-0.5, in1=y2n[:, ct, :], op0=ALU.mult, op1=ALU.subtract
            )
            nc.gpsimd.tensor_tensor(out=t_t[:, 2, :], in0=y4m[:], in1=y2n[:, ct, :], op=ALU.add)
            nc.gpsimd.tensor_tensor(out=t_t[:, 3, :], in0=y4p[:], in1=y2s[:, ct, :], op=ALU.add)
            planes[ct] = t_t

        def last(ct, pieces):
            o_t = fin.tile([P, 4, 8, 2, 8, 2], F32, tag="o", bufs=3)
            images = 4 // pieces
            for h in range(pieces):
                lo, hi = 64 * images * h, 64 * images * (h + 1)
                m0, m1 = images * h, images * (h + 1)
                acc_d = psum.tile([P, 64 * images], F32, tag="ps")
                for g in range(8):
                    mm2(acc_d[:], 0, ct, g, lo, hi)
                for a in range(2):
                    nc.vector.scalar_tensor_tensor(
                        out=o_t[:, m0:m1, :, a].rearrange("p m i j b -> p (m i) j b"),
                        in0=acc_d[:]
                        .rearrange("p (q j) -> p q j", j=8)
                        .unsqueeze(3)
                        .to_broadcast([P, 8 * images, 8, 2]),
                        scalar=0.5,
                        in1=planes[ct][:, 2 * a : 2 * a + 2, lo:hi].rearrange("p b (q j) -> p q j b", j=8),
                        op0=ALU.mult,
                        op1=ALU.add,
                    )
                nc.sync.dma_start(
                    out=out_dram[ct][:, m0:m1, :], in_=o_t[:, m0:m1].rearrange("p m i a j b -> p m (i a j b)")
                )

        for pair in range(2):
            third(2 * pair)
            third(2 * pair + 1)
            last(2 * pair, 1 + pair)
            last(2 * pair + 1, 1 + pair)
